import numpy as np
import ml_dtypes


def mxq(x, axis, fmt="e4m3"):
    dtype, down = {"e4m3": (ml_dtypes.float8_e4m3fn, 7), "e5m2": (ml_dtypes.float8_e5m2, 14)}[fmt]
    v = np.moveaxis(np.asarray(x, np.float32).astype(ml_dtypes.bfloat16).astype(np.float64), axis, -1)
    blocks = v.reshape(v.shape[:-1] + (-1, 32))
    amax = np.abs(blocks).max(-1, keepdims=True)
    byte = np.maximum(np.where(amax > 0, np.frexp(amax)[1] - 1 + 127, 0) - down, 1)
    scale = np.exp2(byte - 127.0)
    codes = (blocks / scale).astype(np.float32).astype(dtype).astype(np.float64)
    return np.moveaxis((codes * scale).reshape(v.shape), -1, axis)


WIDE = False


def mx_kscale(k):
    if not WIDE:
        return np.ones(k)
    levels = np.array([18, -18])
    if k % 512:
        return np.exp2(np.random.permutation(np.resize(levels, k // 32))).repeat(32)
    a = np.empty((k // 512, 16))
    for p in range(k // 512):
        a[p, :8] = np.random.permutation(np.resize(levels, 8))
        for g in range(8):
            far = levels[np.abs(levels - a[p, g]) >= 10]
            a[p, g + 8] = far[np.random.randint(len(far))]
    return np.exp2(a.ravel()).repeat(32)


BF16 = ml_dtypes.bfloat16


def bf(x):
    return np.asarray(x, np.float32).astype(BF16)


def f64(x):
    return np.asarray(x).astype(np.float64)


B, HALF, MID = 512, 512, 2048
D = 2 * HALF


def setup_inputs():
    s = mx_kscale(B)[:, None]
    u = mx_kscale(HALF)
    v = mx_kscale(MID)
    x = bf(np.random.standard_normal((B, D)))
    h3_0 = bf(np.maximum(np.random.standard_normal((B, MID)), 0.0))
    W4_0 = bf(np.random.standard_normal((MID, MID)) * np.sqrt(2.0 / MID))
    b4 = bf(np.random.standard_normal(MID) * 0.2)
    W5_0 = bf(np.random.standard_normal((MID, HALF)) * np.sqrt(2.0 / MID))
    b5 = bf(np.random.standard_normal(HALF) * 0.2)
    z4 = f64(h3_0) @ f64(W4_0) + f64(b4)
    for _ in range(100):
        bad = np.abs(z4).min(axis=1) < 1e-5
        if not bad.any():
            break
        h3_0[bad] = bf(np.maximum(np.random.standard_normal((int(bad.sum()), MID)), 0.0))
        z4[bad] = f64(h3_0[bad]) @ f64(W4_0) + f64(b4)
    g = bf(np.random.standard_normal((B, D)) * np.exp2(np.random.randint(-6, 1, (B, 1))) * 4.0 / s * np.repeat(u, 2))
    return {"x": x,
            "h3": bf(f64(h3_0) * s),
            "W4": bf(f64(W4_0) / v),
            "b4": b4,
            "W5": bf(f64(W5_0) * v[:, None] / u),
            "b5": b5,
            "z4": np.asarray(z4, np.float32),
            "grad_out": g}


def reference(x, h3, W4, b4, W5, b5, z4, grad_out):
    dm = f64(grad_out)[:, 0::2]
    dh = mxq(dm, 1, "e5m2") @ mxq(f64(W5), 1, "e4m3").T
    dz1 = dh * (f64(z4) > 0.0)
    dh3 = mxq(dz1, 1, "e5m2") @ mxq(f64(W4), 1, "e4m3").T
    dW4 = mxq(f64(h3), 0, "e4m3").T @ mxq(dz1, 0, "e5m2")
    return dh3, dW4

@@ -1,0 +1,285 @@
+from contextlib import ExitStack
+
+import concourse.mybir as mybir
+from concourse.masks import make_identity
+
+B, HALF, MID = 512, 512, 2048
+FLOPS = 2 * B * HALF * MID + 2 * (2 * B * MID * MID)
+BYTES = 2 * B * HALF + 2 * MID * HALF + 4 * B * MID + 2 * B * MID + 2 * MID * MID + 4 * B * MID + 4 * MID * MID
+
+F32 = mybir.dt.float32
+BF16 = mybir.dt.bfloat16
+U32 = mybir.dt.uint32
+U8 = mybir.dt.uint8
+E4M3 = mybir.dt.float8_e4m3fn_x4
+E5M2 = mybir.dt.float8_e5m2_x4
+ALU = mybir.AluOpType
+
+P = 128
+J = 4
+N = 512
+STEPS = 16
+LATE_FEATURES = 5
+
+
+def tile_additivecoupling_pa_v_kernel(tc, x, h3, W4, b4, W5, b5, z4, grad_out, out_0, out_1):
+    nc = tc.nc
+    with ExitStack() as ctx:
+        const = ctx.enter_context(tc.tile_pool(name="const", bufs=1))
+        big = ctx.enter_context(tc.tile_pool(name="big", bufs=15))
+        wide = ctx.enter_context(tc.tile_pool(name="wide", bufs=4))
+        small = ctx.enter_context(tc.tile_pool(name="small", bufs=9))
+        psum = ctx.enter_context(tc.psum_pool(name="psum", bufs=4))
+        ctx.enter_context(tc.manual_schedule())
+
+        ident = const.tile([P, P], F32, name="ident")
+        make_identity(nc, ident[:])
+        dz2_codes = const.tile([P, N], U32, name="dz2_codes", align_bytes=64)
+        dz2_scales = const.tile([P, N], U8, name="dz2_scales", align_bytes=64)
+        h3_codes = const.tile([P, MID], U32, name="h3_codes", align_bytes=64)
+        h3_scales = const.tile([P, MID], U8, name="h3_scales", align_bytes=64)
+        tok_codes = const.tile([P, MID], U32, name="tok_codes", align_bytes=64)
+        tok_scales = const.tile([P, MID], U8, name="tok_scales", align_bytes=64)
+        feat_codes = const.tile([P, J, 4, P], U32, name="feat_codes", align_bytes=64)
+        feat_scales = const.tile([P, J, 4, P], U8, name="feat_scales", align_bytes=64)
+
+        def copy(engine, out, in_):
+            if engine == "S":
+                nc.scalar.copy(out=out, in_=in_)
+            else:
+                nc.vector.tensor_copy(out=out, in_=in_)
+
+        def load(shape, dtype, name, source):
+            raw = big.tile(shape, dtype, tag="big", name=name, align_bytes=64)
+            nc.sync.dma_start(out=raw[:], in_=source)
+            return raw
+
+        def quantize(grouped, codes, scales, fmt):
+            nc.vector.quantize_mx(out=codes.bitcast(fmt), scales=scales, in_=grouped[:].rearrange("p c t -> p (c t)"))
+
+        def turn(rows, engines, name):
+            banks = []
+            for pair in range(2):
+                bank = psum.tile([P, 2, 2, P], F32, tag="turned", name="%s_bank_%d" % (name, pair))
+                for i in range(2):
+                    words = rows[2 * pair + i].bitcast(F32)
+                    for u in range(2):
+                        nc.tensor.transpose(bank[:, i, u, :], words[:, u::2], ident[:])
+                banks.append(bank)
+            grouped = small.tile([P, N, J], BF16, tag="grouped", name=name, align_bytes=64)
+            out_words = grouped[:].rearrange("p c t -> p (c t)").bitcast(F32)
+            for pair in range(2):
+                half = out_words[:, N * pair : N * (pair + 1)].rearrange("p (i r u) -> p i r u", i=2, u=2)
+                copy(engines[pair], half, banks[pair][:].rearrange("p i u r -> p i r u"))
+            return grouped
+
+        def interleave(engine, rows, name):
+            grouped = small.tile([P, N, J], BF16, tag="grouped", name=name, align_bytes=64)
+            copy(
+                engine,
+                grouped[:].rearrange("p (c i) t -> p c t i", i=4),
+                rows.rearrange("p t (c i) -> p c t i", i=4),
+            )
+            return grouped
+
+        z4_rows = z4.rearrange("(p j) o -> p j o", j=J)
+        h3_rows = h3.rearrange("(p j) i -> p j i", j=J)
+        raw_w5, raw_z4, raw_h3, raw_w4 = {}, {}, {}, {}
+
+        def load_w5(half):
+            rows = W5[2 * N * half : 2 * N * (half + 1), :].rearrange("(a p j) k -> p a j k", a=2, j=J)
+            raw_w5[half] = load([P, 2, J, HALF], BF16, "raw_w5_%d" % half, rows)
+
+        def load_z4(t):
+            raw_z4[t] = load([P, MID], F32, "raw_z4_%d" % t, z4_rows[:, t, :])
+
+        def load_h3(half):
+            cols = slice(2 * N * half, 2 * N * (half + 1))
+            raw_h3[half] = load([P, J, 2 * N], BF16, "raw_h3_%d" % half, h3_rows[:, :, cols])
+
+        def load_w4(q, half):
+            rows = W4[N * q : N * (q + 1), :].rearrange("(p j) o -> p j o", j=J)
+            raw_w4[q, half] = load([P, 2, MID], BF16, "raw_w4_%d_%d" % (q, half), rows[:, 2 * half : 2 * half + 2, :])
+
+        raw_grad = load([P, J, 2 * HALF], BF16, "raw_grad", grad_out.rearrange("(p j) d -> p j d", j=J))
+        load_w5(0)
+        load_w5(1)
+        load_z4(0)
+        load_z4(1)
+        load_h3(0)
+        load_z4(2)
+        load_z4(3)
+        load_w4(0, 0)
+        load_w4(0, 1)
+        load_h3(1)
+        load_w4(1, 0)
+
+        w5_codes = wide.tile([P, 4, N], U32, tag="wide", name="w5_codes", align_bytes=64)
+        w5_scales = wide.tile([P, 4, N], U8, tag="scales", name="w5_scales", align_bytes=64)
+
+        even = small.tile([P, J, HALF], BF16, tag="grouped", name="even", align_bytes=64)
+        even_cols = raw_grad[:].rearrange("p j (k two) -> p j k two", two=2)[:, :, :, 0]
+        nc.vector.tensor_copy(out=even[:, 0:2, :], in_=even_cols[:, 0:2, :])
+        nc.scalar.copy(out=even[:, 2:J, :], in_=even_cols[:, 2:J, :])
+        dz2_grouped = turn([even[:, j, :] for j in range(J)], "SS", "dz2_grouped")
+        quantize(dz2_grouped, dz2_codes[:], dz2_scales[:], E5M2)
+
+        def turn_w5(a):
+            return turn([raw_w5[a // 2][:, a % 2, j, :] for j in range(J)], "SS", "w5_grouped_%d" % a)
+
+        def quantize_w5(a, grouped):
+            quantize(grouped, w5_codes[:, a, :], w5_scales[:, a, :], E4M3)
+
+        w5_grouped = turn_w5(0)
+        for a in range(1, 4):
+            w5_next = turn_w5(a)
+            quantize_w5(a - 1, w5_grouped)
+            w5_grouped = w5_next
+        quantize_w5(3, w5_grouped)
+
+        dz1 = []
+        for half in range(2):
+            dz1_half = wide.tile([P, J, 2 * N], BF16, tag="wide", name="dz1_%d" % half, align_bytes=64)
+            dz1.append(dz1_half)
+
+        def dz1_chunk(a):
+            return dz1[a // 2][:, :, N * (a % 2) : N * (a % 2 + 1)]
+
+        def make_dz1(t):
+            for a in range(4):
+                dh = psum.tile([P, N], F32, tag="sums", name="dh_%d_%d" % (t, a))
+                nc.tensor.matmul_mx(
+                    out=dh[:],
+                    lhsT=dz2_codes[:, P * t : P * (t + 1)].bitcast(E5M2),
+                    lhsT_scale=dz2_scales[:, P * t : P * (t + 1)],
+                    rhs=w5_codes[:, a, :].bitcast(E4M3),
+                    rhs_scale=w5_scales[:, a, :],
+                    start=True,
+                    stop=True,
+                )
+                nc.vector.scalar_tensor_tensor(
+                    out=dz1_chunk(a)[:, t, :].rearrange("p (m j) -> p m j", j=J),
+                    in0=raw_z4[t][:, N * a : N * (a + 1)].rearrange("p (m j) -> p m j", j=J),
+                    scalar=0.0,
+                    in1=dh[:].rearrange("p (j m) -> p m j", j=J),
+                    op0=ALU.is_gt,
+                    op1=ALU.mult,
+                )
+
+        def turn_dz1(t):
+            return turn([dz1_chunk(g)[:, t, :] for g in range(4)], "SS", "feat_grouped_%d" % t)
+
+        def quantize_feat(t, grouped):
+            codes = feat_codes[:, t, :, :].rearrange("p g r -> p (g r)")
+            scales = feat_scales[:, t, :, :].rearrange("p g r -> p (g r)")
+            quantize(grouped, codes, scales, E5M2)
+
+        def interleave_tok(engine, a):
+            return interleave(engine, dz1_chunk(a), "tok_grouped_%d" % a)
+
+        def quantize_tok(a, grouped):
+            cols = slice(N * a, N * (a + 1))
+            quantize(grouped, tok_codes[:, cols], tok_scales[:, cols], E5M2)
+
+        def interleave_h3(engine, a):
+            return interleave(engine, raw_h3[a // 2][:, :, N * (a % 2) : N * (a % 2 + 1)], "h3_grouped_%d" % a)
+
+        def quantize_h3(a, grouped):
+            cols = slice(N * a, N * (a + 1))
+            quantize(grouped, h3_codes[:, cols], h3_scales[:, cols], E4M3)
+
+        feat_grouped = {}
+        make_dz1(0)
+        make_dz1(1)
+        load_w4(1, 1)
+        h3_grouped = interleave_h3("S", 0)
+        feat_grouped[0] = turn_dz1(0)
+        make_dz1(2)
+        feat_grouped[1] = turn_dz1(1)
+        make_dz1(3)
+        tok_grouped = {0: interleave_tok("S", 0)}
+        load_w4(2, 0)
+        load_w4(2, 1)
+        quantize_h3(0, h3_grouped)
+        feat_grouped[2] = turn_dz1(2)
+        tok_grouped[1] = interleave_tok("V", 1)
+        quantize_tok(0, tok_grouped[0])
+        tok_grouped[3] = interleave_tok("S", 3)
+        tok_grouped[2] = interleave_tok("V", 2)
+        quantize_tok(1, tok_grouped[1])
+        quantize_tok(2, tok_grouped[2])
+        feat_grouped[3] = turn_dz1(3)
+        quantize_tok(3, tok_grouped[3])
+
+        w4_codes, w4_scales = {}, {}
+
+        def turn_w4(unit):
+            q, g = divmod(unit, 4)
+            if g == 0:
+                w4_codes[q] = wide.tile([P, 4, N], U32, tag="wide", name="w4_codes_%d" % q, align_bytes=64)
+                w4_scales[q] = wide.tile([P, 4, N], U8, tag="scales", name="w4_scales_%d" % q, align_bytes=64)
+            rows = [raw_w4[q, j // 2][:, j % 2, N * g : N * (g + 1)] for j in range(J)]
+            return turn(rows, "SS", "w4_grouped_%d" % unit)
+
+        def quantize_w4(unit, grouped):
+            q, g = divmod(unit, 4)
+            quantize(grouped, w4_codes[q][:, g, :], w4_scales[q][:, g, :], E4M3)
+
+        def out_1_tile(s):
+            rows = slice(P * s, P * (s + 1))
+            result = big.tile([P, MID], F32, tag="big", name="out_1_rows_%d" % s, align_bytes=64)
+            for a in range(4):
+                cols = slice(N * a, N * (a + 1))
+                acc = psum.tile([P, N], F32, tag="sums", name="out_1_%d_%d" % (s, a))
+                nc.tensor.matmul_mx(
+                    out=acc[:],
+                    lhsT=h3_codes[:, rows].bitcast(E4M3),
+                    lhsT_scale=h3_scales[:, rows],
+                    rhs=tok_codes[:, cols].bitcast(E5M2),
+                    rhs_scale=tok_scales[:, cols],
+                    start=True,
+                    stop=True,
+                )
+                copy("VS"[a % 2], result[:, cols], acc[:])
+            nc.sync.dma_start(out=out_1[rows, :], in_=result[:])
+
+        for s in range(STEPS):
+            w4_next = turn_w4(s)
+            chunk = s // 4 + 1
+            h3_due = s % 4 == 1 and chunk < 4
+            if h3_due:
+                h3_grouped = interleave_h3("V", chunk)
+            if s > 0:
+                quantize_w4(s - 1, w4_grouped)
+            w4_grouped = w4_next
+            if LATE_FEATURES <= s < LATE_FEATURES + J:
+                quantize_feat(s - LATE_FEATURES, feat_grouped[s - LATE_FEATURES])
+            out_1_tile(s)
+            if s < 2:
+                load_w4(3, s)
+            if h3_due:
+                quantize_h3(chunk, h3_grouped)
+        quantize_w4(STEPS - 1, w4_grouped)
+
+        out_0_rows = out_0.rearrange("(p j) i -> p j i", j=J)
+        for t in range(J):
+            result = big.tile([P, MID], F32, tag="big", name="out_0_rows_%d" % t, align_bytes=64)
+            for q in range(4):
+                acc = psum.tile([P, N], F32, tag="sums", name="out_0_%d_%d" % (t, q))
+                for g in range(4):
+                    nc.tensor.matmul_mx(
+                        out=acc[:],
+                        lhsT=feat_codes[:, t, g, :].bitcast(E5M2),
+                        lhsT_scale=feat_scales[:, t, g, :],
+                        rhs=w4_codes[q][:, g, :].bitcast(E4M3),
+                        rhs_scale=w4_scales[q][:, g, :],
+                        start=(g == 0),
+                        stop=(g == 3),
+                    )
+                cols = slice(N * q, N * (q + 1))
+                copy("SV"[q % 2], result[:, cols].rearrange("p (m j) -> p m j", j=J), acc[:].rearrange("p (j m) -> p m j", j=J))
+                if t == J - 1 and q >= 1:
+                    ready = slice(0 if q == 1 else N * q, N * (q + 1))
+                    nc.sync.dma_start(out=out_0_rows[:, t, ready], in_=result[:, ready])
+            if t < J - 1:
+                nc.sync.dma_start(out=out_0_rows[:, t, :], in_=result[:])

@@ -18,30 +18,45 @@ ALU = mybir.AluOpType
 P = 128
 J = 4
 N = 512
-STEPS = 16
-LATE_FEATURES = 5
+SLOT = 16384
+
+SLOT_W5, SLOT_Z4, SLOT_DZ1, SLOT_H3, SLOT_W4 = 0, 1, 3, 4, 5
 
 
 def tile_additivecoupling_pa_v_kernel(tc, x, h3, W4, b4, W5, b5, z4, grad_out, out_0, out_1):
     nc = tc.nc
     with ExitStack() as ctx:
         const = ctx.enter_context(tc.tile_pool(name="const", bufs=1))
-        big = ctx.enter_context(tc.tile_pool(name="big", bufs=15))
-        wide = ctx.enter_context(tc.tile_pool(name="wide", bufs=4))
-        small = ctx.enter_context(tc.tile_pool(name="small", bufs=9))
-        psum = ctx.enter_context(tc.psum_pool(name="psum", bufs=4))
+        big = ctx.enter_context(tc.tile_pool(name="big", bufs=1))
+        small = ctx.enter_context(tc.tile_pool(name="small", bufs=12))
+        psum = ctx.enter_context(tc.psum_pool(name="psum", bufs=1))
         ctx.enter_context(tc.manual_schedule())
 
         ident = const.tile([P, P], F32, name="ident")
         make_identity(nc, ident[:])
+
+        def mx_tiles(name, tag):
+            codes = const.tile([P, 4, N], U32, tag=tag + "_codes", name=name + "_codes", align_bytes=64)
+            scales = const.tile([P, 4, N], U8, tag=tag + "_scales", name=name + "_scales", align_bytes=64)
+            return codes, scales
+
         dz2_codes = const.tile([P, N], U32, name="dz2_codes", align_bytes=64)
         dz2_scales = const.tile([P, N], U8, name="dz2_scales", align_bytes=64)
-        h3_codes = const.tile([P, MID], U32, name="h3_codes", align_bytes=64)
-        h3_scales = const.tile([P, MID], U8, name="h3_scales", align_bytes=64)
-        tok_codes = const.tile([P, MID], U32, name="tok_codes", align_bytes=64)
-        tok_scales = const.tile([P, MID], U8, name="tok_scales", align_bytes=64)
-        feat_codes = const.tile([P, J, 4, P], U32, name="feat_codes", align_bytes=64)
-        feat_scales = const.tile([P, J, 4, P], U8, name="feat_scales", align_bytes=64)
+        h3_codes, h3_scales = mx_tiles("h3", "h3")
+        tok_codes, tok_scales = mx_tiles("tok", "tok")
+        feat_codes, feat_scales = mx_tiles("feat", "feat")
+        w5_codes, w5_scales = mx_tiles("w5", "last")
+
+        turn_count, sum_count = [], []
+        split = [4]
+
+        def turn_bank(name):
+            turn_count.append(name)
+            return psum.tile([P, 2, 2, P], F32, tag="bank_%d" % (len(turn_count) % split[-1]), name=name)
+
+        def sum_bank(name):
+            sum_count.append(name)
+            return psum.tile([P, N], F32, tag="bank_%d" % (7 - len(sum_count) % (8 - split[-1])), name=name)
 
         def copy(engine, out, in_):
             if engine == "S":
@@ -49,237 +64,331 @@ def tile_additivecoupling_pa_v_kernel(tc, x, h3, W4, b4, W5, b5, z4, grad_out, o
             else:
                 nc.vector.tensor_copy(out=out, in_=in_)
 
-        def load(shape, dtype, name, source):
-            raw = big.tile(shape, dtype, tag="big", name=name, align_bytes=64)
+        def big_tile(shape, dtype, name, offset):
+            return big.tile(shape, dtype, name=name, align_bytes=64, offset=offset)
+
+        def load(shape, dtype, name, offset, source):
+            raw = big_tile(shape, dtype, name, offset)
             nc.sync.dma_start(out=raw[:], in_=source)
             return raw
 
         def quantize(grouped, codes, scales, fmt):
             nc.vector.quantize_mx(out=codes.bitcast(fmt), scales=scales, in_=grouped[:].rearrange("p c t -> p (c t)"))
 
-        def turn(rows, engines, name):
-            banks = []
-            for pair in range(2):
-                bank = psum.tile([P, 2, 2, P], F32, tag="turned", name="%s_bank_%d" % (name, pair))
-                for i in range(2):
-                    words = rows[2 * pair + i].bitcast(F32)
-                    for u in range(2):
-                        nc.tensor.transpose(bank[:, i, u, :], words[:, u::2], ident[:])
-                banks.append(bank)
-            grouped = small.tile([P, N, J], BF16, tag="grouped", name=name, align_bytes=64)
-            out_words = grouped[:].rearrange("p c t -> p (c t)").bitcast(F32)
-            for pair in range(2):
-                half = out_words[:, N * pair : N * (pair + 1)].rearrange("p (i r u) -> p i r u", i=2, u=2)
-                copy(engines[pair], half, banks[pair][:].rearrange("p i u r -> p i r u"))
-            return grouped
+        def new_grouped(name):
+            return small.tile([P, N, J], BF16, tag="grouped", name=name, align_bytes=64)
 
-        def interleave(engine, rows, name):
-            grouped = small.tile([P, N, J], BF16, tag="grouped", name=name, align_bytes=64)
-            copy(
-                engine,
-                grouped[:].rearrange("p (c i) t -> p c t i", i=4),
-                rows.rearrange("p t (c i) -> p c t i", i=4),
-            )
+        def every_second(rows):
+            return [[row.bitcast(F32)[:, u::2] for u in range(2)] for row in rows]
+
+        def turn_words(grouped, pair, words, engine, name):
+            bank = turn_bank("%s_bank_%d" % (name, pair))
+            for i in range(2):
+                for u in range(2):
+                    nc.tensor.transpose(bank[:, i, u, :], words[i][u], ident[:])
+            out_words = grouped[:].rearrange("p c t -> p (c t)").bitcast(F32)
+            half = out_words[:, N * pair : N * (pair + 1)].rearrange("p (i r u) -> p i r u", i=2, u=2)
+            copy(engine, half, bank[:].rearrange("p i u r -> p i r u"))
+
+        def turn_pair(grouped, pair, rows, engine, name):
+            turn_words(grouped, pair, every_second(rows), engine, name)
+
+        def turn(rows, engines, name):
+            grouped = new_grouped(name)
+            for pair in range(2):
+                turn_pair(grouped, pair, rows[2 * pair : 2 * pair + 2], engines[pair], name)
             return grouped
 
         z4_rows = z4.rearrange("(p j) o -> p j o", j=J)
-        h3_rows = h3.rearrange("(p j) i -> p j i", j=J)
-        raw_w5, raw_z4, raw_h3, raw_w4 = {}, {}, {}, {}
+        grad_rows = grad_out.rearrange("(p j) d -> p j d", j=J)
+        raw_grad, raw_w5, raw_z4, raw_w4, raw_w4_whole = {}, {}, {}, {}, {}
 
-        def load_w5(half):
-            rows = W5[2 * N * half : 2 * N * (half + 1), :].rearrange("(a p j) k -> p a j k", a=2, j=J)
-            raw_w5[half] = load([P, 2, J, HALF], BF16, "raw_w5_%d" % half, rows)
+        def load_grad(pair):
+            offset = SLOT * SLOT_DZ1 + SLOT // 4 * pair
+            raw_grad[pair] = load([P, 2, 2 * HALF], BF16, "raw_grad_%d" % pair, offset, grad_rows[:, 2 * pair : 2 * pair + 2, :])
 
-        def load_z4(t):
-            raw_z4[t] = load([P, MID], F32, "raw_z4_%d" % t, z4_rows[:, t, :])
+        def load_w5(first, count):
+            rows = W5[N * first : N * (first + count), :].rearrange("(a p j) k -> p a j k", a=count, j=J)
+            raw = load([P, count, J, HALF], BF16, "raw_w5_%d" % first, SLOT * SLOT_W5 + SLOT // 4 * first, rows)
+            for a in range(count):
+                raw_w5[first + a] = raw[:, a, :, :]
 
-        def load_h3(half):
-            cols = slice(2 * N * half, 2 * N * (half + 1))
-            raw_h3[half] = load([P, J, 2 * N], BF16, "raw_h3_%d" % half, h3_rows[:, :, cols])
+        def load_z4(half, pair):
+            source = z4_rows[:, 2 * pair : 2 * pair + 2, 2 * N * half : 2 * N * (half + 1)]
+            offset = SLOT * SLOT_Z4 + SLOT // 2 * (2 * half + pair)
+            raw_z4[half, pair] = load([P, 2, 2 * N], F32, "raw_z4_%d_%d" % (half, pair), offset, source)
 
-        def load_w4(q, half):
+        def load_w4(q, slot, first, count):
             rows = W4[N * q : N * (q + 1), :].rearrange("(p j) o -> p j o", j=J)
-            raw_w4[q, half] = load([P, 2, MID], BF16, "raw_w4_%d_%d" % (q, half), rows[:, 2 * half : 2 * half + 2, :])
+            offset = SLOT * slot + SLOT // J * first
+            raw = load([P, count, MID], BF16, "raw_w4_%d_%d" % (q, first), offset, rows[:, first : first + count, :])
+            raw_w4_whole[q] = raw
+            for j in range(count):
+                raw_w4[q, first + j] = raw[:, j, :]
 
-        raw_grad = load([P, J, 2 * HALF], BF16, "raw_grad", grad_out.rearrange("(p j) d -> p j d", j=J))
-        load_w5(0)
-        load_w5(1)
-        load_z4(0)
-        load_z4(1)
-        load_h3(0)
-        load_z4(2)
-        load_z4(3)
-        load_w4(0, 0)
-        load_w4(0, 1)
-        load_h3(1)
-        load_w4(1, 0)
+        load_grad(0)
+        load_grad(1)
+        load_w5(0, 1)
+        load_w5(1, 1)
+        load_w5(2, 2)
+        load_z4(0, 0)
+        load_z4(0, 1)
+        load_z4(1, 0)
+        load_z4(1, 1)
+        load_w4(0, SLOT_W4, 0, 2)
+        load_w4(0, SLOT_W4, 2, 2)
+        raw_h3 = load([P, J, MID], BF16, "raw_h3", SLOT * SLOT_H3, h3.rearrange("(p j) i -> p j i", j=J))
+        load_w4(1, SLOT_W4 + 1, 0, 4)
 
-        w5_codes = wide.tile([P, 4, N], U32, tag="wide", name="w5_codes", align_bytes=64)
-        w5_scales = wide.tile([P, 4, N], U8, tag="scales", name="w5_scales", align_bytes=64)
+        dz2_grouped = new_grouped("dz2_grouped")
+        for pair in range(2):
+            even = const.tile([P, 2, HALF], BF16, name="even_%d" % pair, align_bytes=64)
+            even_cols = raw_grad[pair][:].rearrange("p j (k two) -> p j k two", two=2)[:, :, :, 0]
+            nc.vector.tensor_copy(out=even[:], in_=even_cols)
+            turn_pair(dz2_grouped, pair, [even[:, 0, :], even[:, 1, :]], "S", "dz2_grouped")
 
-        even = small.tile([P, J, HALF], BF16, tag="grouped", name="even", align_bytes=64)
-        even_cols = raw_grad[:].rearrange("p j (k two) -> p j k two", two=2)[:, :, :, 0]
-        nc.vector.tensor_copy(out=even[:, 0:2, :], in_=even_cols[:, 0:2, :])
-        nc.scalar.copy(out=even[:, 2:J, :], in_=even_cols[:, 2:J, :])
-        dz2_grouped = turn([even[:, j, :] for j in range(J)], "SS", "dz2_grouped")
-        quantize(dz2_grouped, dz2_codes[:], dz2_scales[:], E5M2)
-
-        def turn_w5(a):
-            return turn([raw_w5[a // 2][:, a % 2, j, :] for j in range(J)], "SS", "w5_grouped_%d" % a)
-
+        def turn_w5(a, engines):
+            return turn([raw_w5[a][:, j, :] for j in range(J)], engines, "w5_grouped_%d" % a)
         def quantize_w5(a, grouped):
             quantize(grouped, w5_codes[:, a, :], w5_scales[:, a, :], E4M3)
 
-        w5_grouped = turn_w5(0)
-        for a in range(1, 4):
-            w5_next = turn_w5(a)
-            quantize_w5(a - 1, w5_grouped)
-            w5_grouped = w5_next
-        quantize_w5(3, w5_grouped)
+        dz1 = {}
 
-        dz1 = []
-        for half in range(2):
-            dz1_half = wide.tile([P, J, 2 * N], BF16, tag="wide", name="dz1_%d" % half, align_bytes=64)
-            dz1.append(dz1_half)
-
-        def dz1_chunk(a):
-            return dz1[a // 2][:, :, N * (a % 2) : N * (a % 2 + 1)]
-
-        def make_dz1(t):
-            for a in range(4):
-                dh = psum.tile([P, N], F32, tag="sums", name="dh_%d_%d" % (t, a))
-                nc.tensor.matmul_mx(
-                    out=dh[:],
-                    lhsT=dz2_codes[:, P * t : P * (t + 1)].bitcast(E5M2),
-                    lhsT_scale=dz2_scales[:, P * t : P * (t + 1)],
-                    rhs=w5_codes[:, a, :].bitcast(E4M3),
-                    rhs_scale=w5_scales[:, a, :],
-                    start=True,
-                    stop=True,
-                )
-                nc.vector.scalar_tensor_tensor(
-                    out=dz1_chunk(a)[:, t, :].rearrange("p (m j) -> p m j", j=J),
-                    in0=raw_z4[t][:, N * a : N * (a + 1)].rearrange("p (m j) -> p m j", j=J),
-                    scalar=0.0,
-                    in1=dh[:].rearrange("p (j m) -> p m j", j=J),
-                    op0=ALU.is_gt,
-                    op1=ALU.mult,
-                )
-
-        def turn_dz1(t):
-            return turn([dz1_chunk(g)[:, t, :] for g in range(4)], "SS", "feat_grouped_%d" % t)
-
-        def quantize_feat(t, grouped):
-            codes = feat_codes[:, t, :, :].rearrange("p g r -> p (g r)")
-            scales = feat_scales[:, t, :, :].rearrange("p g r -> p (g r)")
-            quantize(grouped, codes, scales, E5M2)
-
-        def interleave_tok(engine, a):
-            return interleave(engine, dz1_chunk(a), "tok_grouped_%d" % a)
-
-        def quantize_tok(a, grouped):
-            cols = slice(N * a, N * (a + 1))
-            quantize(grouped, tok_codes[:, cols], tok_scales[:, cols], E5M2)
-
-        def interleave_h3(engine, a):
-            return interleave(engine, raw_h3[a // 2][:, :, N * (a % 2) : N * (a % 2 + 1)], "h3_grouped_%d" % a)
-
-        def quantize_h3(a, grouped):
-            cols = slice(N * a, N * (a + 1))
-            quantize(grouped, h3_codes[:, cols], h3_scales[:, cols], E4M3)
+        def make_dz1(a, t):
+            if a not in dz1:
+                dz1[a] = big_tile([P, J, N], BF16, "dz1_%d" % a, SLOT * SLOT_DZ1 + SLOT // 4 * a)
+            dh = sum_bank("dh_%d_%d" % (a, t))
+            nc.tensor.matmul_mx(
+                out=dh[:],
+                lhsT=dz2_codes[:, P * t : P * (t + 1)].bitcast(E5M2),
+                lhsT_scale=dz2_scales[:, P * t : P * (t + 1)],
+                rhs=w5_codes[:, a, :].bitcast(E4M3),
+                rhs_scale=w5_scales[:, a, :],
+                start=True,
+                stop=True,
+            )
+            saved = raw_z4[a // 2, t // 2][:, t % 2, N * (a % 2) : N * (a % 2 + 1)]
+            nc.vector.scalar_tensor_tensor(
+                out=dz1[a][:, t, :].rearrange("p (m j) -> p m j", j=J),
+                in0=saved.rearrange("p (m j) -> p m j", j=J),
+                scalar=0.0,
+                in1=dh[:].rearrange("p (j m) -> p m j", j=J),
+                op0=ALU.is_gt,
+                op1=ALU.mult,
+            )
 
         feat_grouped = {}
-        make_dz1(0)
-        make_dz1(1)
-        load_w4(1, 1)
-        h3_grouped = interleave_h3("S", 0)
-        feat_grouped[0] = turn_dz1(0)
-        make_dz1(2)
-        feat_grouped[1] = turn_dz1(1)
-        make_dz1(3)
-        tok_grouped = {0: interleave_tok("S", 0)}
-        load_w4(2, 0)
-        load_w4(2, 1)
-        quantize_h3(0, h3_grouped)
-        feat_grouped[2] = turn_dz1(2)
-        tok_grouped[1] = interleave_tok("V", 1)
-        quantize_tok(0, tok_grouped[0])
-        tok_grouped[3] = interleave_tok("S", 3)
-        tok_grouped[2] = interleave_tok("V", 2)
-        quantize_tok(1, tok_grouped[1])
-        quantize_tok(2, tok_grouped[2])
-        feat_grouped[3] = turn_dz1(3)
-        quantize_tok(3, tok_grouped[3])
 
-        w4_codes, w4_scales = {}, {}
+        def turn_dz1(half, pair, engines="SS"):
+            for a in (2 * half, 2 * half + 1):
+                if pair == 0:
+                    feat_grouped[a] = new_grouped("feat_grouped_%d" % a)
+                rows = [dz1[a][:, t, :] for t in (2 * pair, 2 * pair + 1)]
+                turn_pair(feat_grouped[a], pair, rows, engines[a % 2], "feat_grouped_%d" % a)
 
-        def turn_w4(unit):
-            q, g = divmod(unit, 4)
+        def make_dz1_part(half, pair):
+            for a in (2 * half, 2 * half + 1):
+                for t in (2 * pair, 2 * pair + 1):
+                    make_dz1(a, t)
+
+        def quantize_feat(a):
+            quantize(feat_grouped[a], feat_codes[:, a, :], feat_scales[:, a, :], E5M2)
+
+        tok_grouped = {}
+
+        def interleave_tok(engine, a, part=0, parts=1):
+            if part == 0:
+                tok_grouped[a] = new_grouped("tok_grouped_%d" % a)
+            cols = slice(N // parts * part, N // parts * (part + 1))
+            out = tok_grouped[a][:, cols, :].rearrange("p (c i) t -> p c t i", i=4)
+            copy(engine, out, dz1[a][:, :, cols].rearrange("p t (c i) -> p c t i", i=4))
+
+        def quantize_tok(a):
+            quantize(tok_grouped[a], tok_codes[:, a, :], tok_scales[:, a, :], E5M2)
+
+        h3_grouped = {}
+
+        def interleave_h3(engine, r, part=0, parts=1):
+            if part == 0:
+                h3_grouped[r] = new_grouped("h3_grouped_%d" % r)
+            ms = slice(P // parts * part, P // parts * (part + 1))
+            source = raw_h3[:, :, N * r : N * (r + 1)].rearrange("p t (m e) -> p m t e", e=4)
+            copy(engine, h3_grouped[r][:].rearrange("p (e m) t -> p m t e", e=4)[:, ms, :, :], source[:, ms, :, :])
+
+        def quantize_h3(r):
+            quantize(h3_grouped[r], h3_codes[:, r, :], h3_scales[:, r, :], E4M3)
+
+        w4_codes, w4_scales, w4_grouped = {}, {}, {}
+
+        w4_sorted = {}
+
+        def sort_w4(q, g):
+            words = small.tile([P, J, 2, P], F32, tag="grouped", name="w4_sorted_%d_%d" % (q, g), align_bytes=64)
+            source = raw_w4_whole[q][:, :, N * g : N * (g + 1)].bitcast(F32)
+            nc.vector.tensor_copy(out=words[:], in_=source.rearrange("p j (w u) -> p j u w", u=2))
+            w4_sorted[q, g] = words
+
+        def turn_w4(q, g, pairs=(0, 1), engines="SS"):
+            name = "w4_grouped_%d_%d" % (q, g)
+            if (q, g) not in w4_grouped:
+                w4_grouped[q, g] = new_grouped(name)
+            for pair in pairs:
+                if (q, g) in w4_sorted:
+                    words = [[w4_sorted[q, g][:, j, u, :] for u in range(2)] for j in (2 * pair, 2 * pair + 1)]
+                else:
+                    words = every_second([raw_w4[q, j][:, N * g : N * (g + 1)] for j in (2 * pair, 2 * pair + 1)])
+                turn_words(w4_grouped[q, g], pair, words, engines[pair], name)
+
+        def quantize_w4(q, g):
+            if q not in w4_codes:
+                w4_codes[q], w4_scales[q] = mx_tiles("w4_%d" % q, "last" if q == 3 else "w4_%d" % q)
+            quantize(w4_grouped[q, g], w4_codes[q][:, g, :], w4_scales[q][:, g, :], E4M3)
+
+        out_1_rows = out_1.rearrange("(r p e) o -> r p e o", p=P, e=J)
+        out_0_rows = out_0.rearrange("(p t) i -> p t i", t=J)
+        staged_1, staged_0 = {}, {}
+
+        def out_1_bank(s, a, engine, slot):
+            r, e = divmod(s, J)
+            if s // 2 not in staged_1:
+                staged_1[s // 2] = big_tile([P, 2, MID], F32, "out_1_rows_%d" % (s // 2), SLOT * slot)
+            acc = sum_bank("out_1_%d_%d" % (s, a))
+            nc.tensor.matmul_mx(
+                out=acc[:],
+                lhsT=h3_codes[:, r, P * e : P * (e + 1)].bitcast(E4M3),
+                lhsT_scale=h3_scales[:, r, P * e : P * (e + 1)],
+                rhs=tok_codes[:, a, :].bitcast(E5M2),
+                rhs_scale=tok_scales[:, a, :],
+                start=True,
+                stop=True,
+            )
+            copy(engine, staged_1[s // 2][:, e % 2, N * a : N * (a + 1)], acc[:])
+
+        def store_out_1(s, count):
+            r, e = divmod(s, J)
+            nc.sync.dma_start(out=out_1_rows[r, :, e : e + count, :], in_=staged_1[s // 2][:, e % 2 : e % 2 + count, :])
+
+        open_sums = {}
+
+        def out_0_pass(t, q, g):
             if g == 0:
-                w4_codes[q] = wide.tile([P, 4, N], U32, tag="wide", name="w4_codes_%d" % q, align_bytes=64)
-                w4_scales[q] = wide.tile([P, 4, N], U8, tag="scales", name="w4_scales_%d" % q, align_bytes=64)
-            rows = [raw_w4[q, j // 2][:, j % 2, N * g : N * (g + 1)] for j in range(J)]
-            return turn(rows, "SS", "w4_grouped_%d" % unit)
+                open_sums[t, q] = sum_bank("out_0_%d_%d" % (t, q))
+            nc.tensor.matmul_mx(
+                out=open_sums[t, q][:],
+                lhsT=feat_codes[:, g, P * t : P * (t + 1)].bitcast(E5M2),
+                lhsT_scale=feat_scales[:, g, P * t : P * (t + 1)],
+                rhs=w4_codes[q][:, g, :].bitcast(E4M3),
+                rhs_scale=w4_scales[q][:, g, :],
+                start=(g == 0),
+                stop=(g == 3),
+            )
 
-        def quantize_w4(unit, grouped):
-            q, g = divmod(unit, 4)
-            quantize(grouped, w4_codes[q][:, g, :], w4_scales[q][:, g, :], E4M3)
+        def out_0_copy(t, q, engine):
+            if q not in staged_0:
+                staged_0[q] = big_tile([P, J, N], F32, "out_0_cols_%d" % q, SLOT * SLOT_W4 + SLOT // 2 * (q % 2))
+            rows = staged_0[q][:, t, :]
+            copy(engine, rows.rearrange("p (m j) -> p m j", j=J), open_sums[t, q][:].rearrange("p (j m) -> p m j", j=J))
 
-        def out_1_tile(s):
-            rows = slice(P * s, P * (s + 1))
-            result = big.tile([P, MID], F32, tag="big", name="out_1_rows_%d" % s, align_bytes=64)
+        def out_0_bank(t, q, engine):
+            for g in range(4):
+                out_0_pass(t, q, g)
+            out_0_copy(t, q, engine)
+
+        def store_out_0(q, first, count):
+            tiles = slice(first, first + count)
+            nc.sync.dma_start(out=out_0_rows[:, tiles, N * q : N * (q + 1)], in_=staged_0[q][:, tiles, :])
+
+        w5_grouped = {0: turn_w5(0, "VS")}
+        quantize(dz2_grouped, dz2_codes[:], dz2_scales[:], E5M2)
+        w5_grouped[1] = turn_w5(1, "VS")
+        quantize_w5(0, w5_grouped[0])
+        w5_grouped[2] = turn_w5(2, "SS")
+        quantize_w5(1, w5_grouped[1])
+        w5_grouped[3] = turn_w5(3, "SS")
+        load_w4(2, SLOT_W5, 0, 4)
+        quantize_w5(2, w5_grouped[2])
+        make_dz1_part(0, 0)
+        quantize_w5(3, w5_grouped[3])
+        make_dz1_part(0, 1)
+        turn_dz1(0, 0)
+        make_dz1_part(1, 0)
+        interleave_tok("S", 0, 0, 2)
+        turn_dz1(0, 1)
+        interleave_tok("S", 0, 1, 2)
+        make_dz1_part(1, 1)
+        load_w4(3, SLOT_Z4, 0, 4)
+        turn_dz1(1, 0)
+        interleave_tok("V", 1)
+        turn_w4(0, 0)
+        quantize_tok(0)
+        turn_dz1(1, 1)
+        interleave_tok("V", 2)
+        quantize_tok(1)
+        turn_w4(0, 1)
+        interleave_tok("V", 3)
+        turn_w4(0, 2)
+        interleave_h3("V", 0)
+        quantize_tok(2)
+        quantize_h3(0)
+        quantize_tok(3)
+        turn_w4(0, 3)
+        interleave_h3("S", 1, 0, 2)
+
+        slots = [SLOT_Z4 + 1, SLOT_DZ1, SLOT_W4 + 1, SLOT_Z4 + 1, SLOT_DZ1, SLOT_W4 + 1, SLOT_W5, SLOT_H3]
+        split.append(2)
+
+        def out_1_tile(s, engines="VSVS"):
             for a in range(4):
-                cols = slice(N * a, N * (a + 1))
-                acc = psum.tile([P, N], F32, tag="sums", name="out_1_%d_%d" % (s, a))
-                nc.tensor.matmul_mx(
-                    out=acc[:],
-                    lhsT=h3_codes[:, rows].bitcast(E4M3),
-                    lhsT_scale=h3_scales[:, rows],
-                    rhs=tok_codes[:, cols].bitcast(E5M2),
-                    rhs_scale=tok_scales[:, cols],
-                    start=True,
-                    stop=True,
-                )
-                copy("VS"[a % 2], result[:, cols], acc[:])
-            nc.sync.dma_start(out=out_1[rows, :], in_=result[:])
+                out_1_bank(s, a, engines[a], slots[s // 2])
+            if s % 2 == 1:
+                store_out_1(s - 1, 2)
 
-        for s in range(STEPS):
-            w4_next = turn_w4(s)
-            chunk = s // 4 + 1
-            h3_due = s % 4 == 1 and chunk < 4
-            if h3_due:
-                h3_grouped = interleave_h3("V", chunk)
-            if s > 0:
-                quantize_w4(s - 1, w4_grouped)
-            w4_grouped = w4_next
-            if LATE_FEATURES <= s < LATE_FEATURES + J:
-                quantize_feat(s - LATE_FEATURES, feat_grouped[s - LATE_FEATURES])
-            out_1_tile(s)
-            if s < 2:
-                load_w4(3, s)
-            if h3_due:
-                quantize_h3(chunk, h3_grouped)
-        quantize_w4(STEPS - 1, w4_grouped)
+        def finish_out_0(i, engine):
+            out_0_copy(i % 4, i // 4, engine)
+            if i % 4 == 3:
+                store_out_0(i // 4, 0, 4)
 
-        out_0_rows = out_0.rearrange("(p j) i -> p j i", j=J)
-        for t in range(J):
-            result = big.tile([P, MID], F32, tag="big", name="out_0_rows_%d" % t, align_bytes=64)
-            for q in range(4):
-                acc = psum.tile([P, N], F32, tag="sums", name="out_0_%d_%d" % (t, q))
-                for g in range(4):
-                    nc.tensor.matmul_mx(
-                        out=acc[:],
-                        lhsT=feat_codes[:, t, g, :].bitcast(E5M2),
-                        lhsT_scale=feat_scales[:, t, g, :],
-                        rhs=w4_codes[q][:, g, :].bitcast(E4M3),
-                        rhs_scale=w4_scales[q][:, g, :],
-                        start=(g == 0),
-                        stop=(g == 3),
-                    )
-                cols = slice(N * q, N * (q + 1))
-                copy("SV"[q % 2], result[:, cols].rearrange("p (m j) -> p m j", j=J), acc[:].rearrange("p (j m) -> p m j", j=J))
-                if t == J - 1 and q >= 1:
-                    ready = slice(0 if q == 1 else N * q, N * (q + 1))
-                    nc.sync.dma_start(out=out_0_rows[:, t, ready], in_=result[:, ready])
-            if t < J - 1:
-                nc.sync.dma_start(out=out_0_rows[:, t, :], in_=result[:])
+        FIRST_SORTED, FIRST_MIXED = 7, 7
+        for s in range(2):
+            quantize_feat(s)
+            quantize_w4(0, s)
+            out_1_tile(s, "SSVS")
+        for unit in range(4, 16):
+            q, g = divmod(unit, 4)
+            s = unit - 2
+            q0, t0 = divmod(unit - FIRST_MIXED, 4)
+            turn_w4(q, g)
+            if unit > FIRST_MIXED:
+                finish_out_0(unit - 1 - FIRST_MIXED, "V")
+            if FIRST_SORTED <= unit + 1 < 16:
+                sort_w4(*divmod(unit + 1, 4))
+            if unit in (5, 6):
+                quantize_w4(0, unit - 3)
+            if unit == 5:
+                quantize_feat(3)
+            for a in range(4):
+                out_1_bank(s, a, ("VSSS" if unit >= FIRST_MIXED else "SVSS")[a], slots[s // 2])
+                if unit >= FIRST_MIXED:
+                    out_0_pass(t0, q0, a)
+                if a == 0 and unit > 4:
+                    quantize_w4(*divmod(unit - 1, 4))
+            if s % 2 == 1:
+                store_out_1(s - 1, 2)
+            if unit == 4:
+                interleave_h3("V", 1, 1, 2)
+                quantize_feat(2)
+                quantize_h3(1)
+            if unit in (7, 8, 11, 12):
+                interleave_h3("V", (unit + 1) // 4, (unit + 1) % 4, 2)
+            if unit in (9, 13):
+                quantize_h3(q)
+        quantize_w4(3, 3)
+        done = 16 - FIRST_MIXED
+        finish_out_0(done - 1, "V")
+        split.append(0)
+        for i in range(done, 16):
+            if i - done < 2:
+                out_1_tile(14 + i - done)
+            for g in range(4):
+                out_0_pass(i % 4, i // 4, g)
+            finish_out_0(i, "SV"[i % 2])

@@ -208,12 +208,13 @@ def tile_additivecoupling_pa_v_kernel(tc, x, h3, W4, b4, W5, b5, z4, grad_out, o
 
         h3_grouped = {}
 
-        def interleave_h3(engine, r, part=0, parts=1):
-            if part == 0:
+        def interleave_h3(engine, r, half):
+            if half == 0:
                 h3_grouped[r] = new_grouped("h3_grouped_%d" % r)
-            ms = slice(P // parts * part, P // parts * (part + 1))
-            source = raw_h3[:, :, N * r : N * (r + 1)].rearrange("p t (m e) -> p m t e", e=4)
-            copy(engine, h3_grouped[r][:].rearrange("p (e m) t -> p m t e", e=4)[:, ms, :, :], source[:, ms, :, :])
+            cols = slice(N // 2 * half, N // 2 * (half + 1))
+            source = raw_h3[:, :, N * r : N * (r + 1)][:, :, cols]
+            out = h3_grouped[r][:, cols, :].rearrange("p (e m i) t -> p m t i e", e=2, i=2)
+            copy(engine, out, source.rearrange("p t (m i e) -> p m t i e", e=2, i=2))
 
         def quantize_h3(r):
             quantize(h3_grouped[r], h3_codes[:, r, :], h3_scales[:, r, :], E4M3)
@@ -244,7 +245,7 @@ def tile_additivecoupling_pa_v_kernel(tc, x, h3, W4, b4, W5, b5, z4, grad_out, o
                 w4_codes[q], w4_scales[q] = mx_tiles("w4_%d" % q, "last" if q == 3 else "w4_%d" % q)
             quantize(w4_grouped[q, g], w4_codes[q][:, g, :], w4_scales[q][:, g, :], E4M3)
 
-        out_1_rows = out_1.rearrange("(r p e) o -> r p e o", p=P, e=J)
+        out_1_rows = out_1.rearrange("(r p e) o -> r p e o", p=P, e=2)
         out_0_rows = out_0.rearrange("(p t) i -> p t i", t=J)
         staged_1, staged_0 = {}, {}
 
@@ -265,8 +266,8 @@ def tile_additivecoupling_pa_v_kernel(tc, x, h3, W4, b4, W5, b5, z4, grad_out, o
             copy(engine, staged_1[s // 2][:, e % 2, N * a : N * (a + 1)], acc[:])
 
         def store_out_1(s, count):
-            r, e = divmod(s, J)
-            nc.sync.dma_start(out=out_1_rows[r, :, e : e + count, :], in_=staged_1[s // 2][:, e % 2 : e % 2 + count, :])
+            r, e = divmod(s, 2)
+            nc.sync.dma_start(out=out_1_rows[r, :, e : e + count, :], in_=staged_1[r][:, e : e + count, :])
 
         open_sums = {}
 
@@ -327,12 +328,13 @@ def tile_additivecoupling_pa_v_kernel(tc, x, h3, W4, b4, W5, b5, z4, grad_out, o
         turn_w4(0, 1)
         interleave_tok("V", 3)
         turn_w4(0, 2)
-        interleave_h3("V", 0)
+        interleave_h3("V", 0, 0)
+        interleave_h3("V", 0, 1)
         quantize_tok(2)
         quantize_h3(0)
         quantize_tok(3)
         turn_w4(0, 3)
-        interleave_h3("S", 1, 0, 2)
+        interleave_h3("S", 1, 0)
 
         slots = [SLOT_Z4 + 1, SLOT_DZ1, SLOT_W4 + 1, SLOT_Z4 + 1, SLOT_DZ1, SLOT_W4 + 1, SLOT_W5, SLOT_H3]
         split.append(2)
@@ -368,18 +370,19 @@ def tile_additivecoupling_pa_v_kernel(tc, x, h3, W4, b4, W5, b5, z4, grad_out, o
                 quantize_feat(3)
             for a in range(4):
                 out_1_bank(s, a, ("VSSS" if unit >= FIRST_MIXED else "SVSS")[a], slots[s // 2])
-                if unit >= FIRST_MIXED:
-                    out_0_pass(t0, q0, a)
                 if a == 0 and unit > 4:
                     quantize_w4(*divmod(unit - 1, 4))
+            if unit >= FIRST_MIXED:
+                for a in range(4):
+                    out_0_pass(t0, q0, a)
             if s % 2 == 1:
                 store_out_1(s - 1, 2)
             if unit == 4:
-                interleave_h3("V", 1, 1, 2)
+                interleave_h3("V", 1, 1)
                 quantize_feat(2)
                 quantize_h3(1)
             if unit in (7, 8, 11, 12):
-                interleave_h3("V", (unit + 1) // 4, (unit + 1) % 4, 2)
+                interleave_h3("V", (unit + 1) // 4, (unit + 1) % 4)
             if unit in (9, 13):
                 quantize_h3(q)
         quantize_w4(3, 3)

@@ -342,13 +342,19 @@ def tile_additivecoupling_pa_v_kernel(tc, x, h3, W4, b4, W5, b5, z4, grad_out, o
         def out_1_tile(s, engines="VSVS"):
             for a in range(4):
                 out_1_bank(s, a, engines[a], slots[s // 2])
-            if s % 2 == 1:
+            if s >= 4:
+                store_out_1(s, 1)
+            elif s % 2 == 1:
                 store_out_1(s - 1, 2)
 
         def finish_out_0(i, engine):
             out_0_copy(i % 4, i // 4, engine)
-            if i % 4 == 3:
+            if i % 4 == 3 and i < 12:
                 store_out_0(i // 4, 0, 4)
+            if i == 13:
+                store_out_0(3, 0, 2)
+            if i > 13:
+                store_out_0(3, i % 4, 1)
 
         FIRST_SORTED, FIRST_MIXED = 7, 7
         for s in range(2):
@@ -375,7 +381,9 @@ def tile_additivecoupling_pa_v_kernel(tc, x, h3, W4, b4, W5, b5, z4, grad_out, o
             if unit >= FIRST_MIXED:
                 for a in range(4):
                     out_0_pass(t0, q0, a)
-            if s % 2 == 1:
+            if s >= 4:
+                store_out_1(s, 1)
+            elif s % 2 == 1:
                 store_out_1(s - 1, 2)
             if unit == 4:
                 interleave_h3("V", 1, 1)

@@ -47,16 +47,17 @@ def tile_additivecoupling_pa_v_kernel(tc, x, h3, W4, b4, W5, b5, z4, grad_out, o
         feat_codes, feat_scales = mx_tiles("feat", "feat")
         w5_codes, w5_scales = mx_tiles("w5", "last")
 
-        turn_count, sum_count = [], []
-        split = [4]
+        banks_taken = []
+
+        def next_bank(shape, name):
+            banks_taken.append(name)
+            return psum.tile(shape, F32, tag="bank_%d" % (len(banks_taken) % 8), name=name)
 
         def turn_bank(name):
-            turn_count.append(name)
-            return psum.tile([P, 2, 2, P], F32, tag="bank_%d" % (len(turn_count) % split[-1]), name=name)
+            return next_bank([P, 2, 2, P], name)
 
         def sum_bank(name):
-            sum_count.append(name)
-            return psum.tile([P, N], F32, tag="bank_%d" % (7 - len(sum_count) % (8 - split[-1])), name=name)
+            return next_bank([P, N], name)
 
         def copy(engine, out, in_):
             if engine == "S":
@@ -135,9 +136,9 @@ def tile_additivecoupling_pa_v_kernel(tc, x, h3, W4, b4, W5, b5, z4, grad_out, o
         load_z4(0, 1)
         load_z4(1, 0)
         load_z4(1, 1)
+        raw_h3 = load([P, J, MID], BF16, "raw_h3", SLOT * SLOT_H3, h3.rearrange("(p j) i -> p j i", j=J))
         load_w4(0, SLOT_W4, 0, 2)
         load_w4(0, SLOT_W4, 2, 2)
-        raw_h3 = load([P, J, MID], BF16, "raw_h3", SLOT * SLOT_H3, h3.rearrange("(p j) i -> p j i", j=J))
         load_w4(1, SLOT_W4 + 1, 0, 4)
 
         dz2_grouped = new_grouped("dz2_grouped")
@@ -179,17 +180,12 @@ def tile_additivecoupling_pa_v_kernel(tc, x, h3, W4, b4, W5, b5, z4, grad_out, o
 
         feat_grouped = {}
 
-        def turn_dz1(half, pair, engines="SS"):
-            for a in (2 * half, 2 * half + 1):
-                if pair == 0:
-                    feat_grouped[a] = new_grouped("feat_grouped_%d" % a)
-                rows = [dz1[a][:, t, :] for t in (2 * pair, 2 * pair + 1)]
-                turn_pair(feat_grouped[a], pair, rows, engines[a % 2], "feat_grouped_%d" % a)
+        def turn_dz1(a, engines="SS"):
+            feat_grouped[a] = turn([dz1[a][:, t, :] for t in range(J)], engines, "feat_grouped_%d" % a)
 
-        def make_dz1_part(half, pair):
-            for a in (2 * half, 2 * half + 1):
-                for t in (2 * pair, 2 * pair + 1):
-                    make_dz1(a, t)
+        def make_dz1_chunk(a):
+            for t in range(J):
+                make_dz1(a, t)
 
         def quantize_feat(a):
             quantize(feat_grouped[a], feat_codes[:, a, :], feat_scales[:, a, :], E5M2)
@@ -249,10 +245,10 @@ def tile_additivecoupling_pa_v_kernel(tc, x, h3, W4, b4, W5, b5, z4, grad_out, o
         out_0_rows = out_0.rearrange("(p t) i -> p t i", t=J)
         staged_1, staged_0 = {}, {}
 
-        def out_1_bank(s, a, engine, slot):
+        def out_1_bank(s, a, engine, half_slot):
             r, e = divmod(s, J)
-            if s // 2 not in staged_1:
-                staged_1[s // 2] = big_tile([P, 2, MID], F32, "out_1_rows_%d" % (s // 2), SLOT * slot)
+            if s not in staged_1:
+                staged_1[s] = big_tile([P, MID], F32, "out_1_rows_%d" % s, SLOT // 2 * half_slot)
             acc = sum_bank("out_1_%d_%d" % (s, a))
             nc.tensor.matmul_mx(
                 out=acc[:],
@@ -263,11 +259,10 @@ def tile_additivecoupling_pa_v_kernel(tc, x, h3, W4, b4, W5, b5, z4, grad_out, o
                 start=True,
                 stop=True,
             )
-            copy(engine, staged_1[s // 2][:, e % 2, N * a : N * (a + 1)], acc[:])
+            copy(engine, staged_1[s][:, N * a : N * (a + 1)], acc[:])
 
-        def store_out_1(s, count):
-            r, e = divmod(s, 2)
-            nc.sync.dma_start(out=out_1_rows[r, :, e : e + count, :], in_=staged_1[r][:, e : e + count, :])
+        def store_out_1(s):
+            nc.sync.dma_start(out=out_1_rows[s // 2, :, s % 2, :], in_=staged_1[s][:])
 
         open_sums = {}
 
@@ -305,47 +300,47 @@ def tile_additivecoupling_pa_v_kernel(tc, x, h3, W4, b4, W5, b5, z4, grad_out, o
         quantize_w5(0, w5_grouped[0])
         w5_grouped[2] = turn_w5(2, "SS")
         quantize_w5(1, w5_grouped[1])
+        make_dz1(0, 0)
+        make_dz1(0, 1)
         w5_grouped[3] = turn_w5(3, "SS")
         load_w4(2, SLOT_W5, 0, 4)
         quantize_w5(2, w5_grouped[2])
-        make_dz1_part(0, 0)
+        make_dz1(0, 2)
+        make_dz1(0, 3)
+        make_dz1_chunk(1)
+        interleave_tok("S", 0)
+        turn_dz1(0)
         quantize_w5(3, w5_grouped[3])
-        make_dz1_part(0, 1)
-        turn_dz1(0, 0)
-        make_dz1_part(1, 0)
-        interleave_tok("S", 0, 0, 2)
-        turn_dz1(0, 1)
-        interleave_tok("S", 0, 1, 2)
-        make_dz1_part(1, 1)
+        make_dz1_chunk(2)
+        interleave_tok("S", 1, 0, 2)
+        turn_dz1(1)
+        make_dz1_chunk(3)
         load_w4(3, SLOT_Z4, 0, 4)
-        turn_dz1(1, 0)
-        interleave_tok("V", 1)
-        turn_w4(0, 0)
-        quantize_tok(0)
-        turn_dz1(1, 1)
+        turn_dz1(2)
+        interleave_tok("V", 1, 1, 2)
         interleave_tok("V", 2)
-        quantize_tok(1)
-        turn_w4(0, 1)
+        turn_dz1(3)
+        interleave_h3("S", 0, 0)
+        quantize_tok(0)
         interleave_tok("V", 3)
-        turn_w4(0, 2)
-        interleave_h3("V", 0, 0)
+        for g in range(4):
+            turn_w4(0, g, (0,))
+        quantize_tok(1)
         interleave_h3("V", 0, 1)
         quantize_tok(2)
         quantize_h3(0)
         quantize_tok(3)
-        turn_w4(0, 3)
-        interleave_h3("S", 1, 0)
+        for g in range(4):
+            turn_w4(0, g, (1,))
+        interleave_h3("V", 1, 0)
 
-        slots = [SLOT_Z4 + 1, SLOT_DZ1, SLOT_W4 + 1, SLOT_Z4 + 1, SLOT_DZ1, SLOT_W4 + 1, SLOT_W5, SLOT_H3]
-        split.append(2)
+        Z, D, W, H = 2 * SLOT_Z4 + 2, 2 * SLOT_DZ1, 2 * SLOT_W4, 2 * SLOT_H3
+        halves = [Z, Z + 1, D, D + 1, W + 1, W + 2, W + 3, Z, Z + 1, D, D + 1, W + 2, W + 3, 0, 1, H]
 
         def out_1_tile(s, engines="VSVS"):
             for a in range(4):
-                out_1_bank(s, a, engines[a], slots[s // 2])
-            if s >= 4:
-                store_out_1(s, 1)
-            elif s % 2 == 1:
-                store_out_1(s - 1, 2)
+                out_1_bank(s, a, engines[a], halves[s])
+            store_out_1(s)
 
         def finish_out_0(i, engine):
             out_0_copy(i % 4, i // 4, engine)
@@ -356,16 +351,23 @@ def tile_additivecoupling_pa_v_kernel(tc, x, h3, W4, b4, W5, b5, z4, grad_out, o
             if i > 13:
                 store_out_0(3, i % 4, 1)
 
-        FIRST_SORTED, FIRST_MIXED = 7, 7
+        FIRST_SORTED, FIRST_MIXED, TWO_TILES = 8, 7, (9, 13)
         for s in range(2):
             quantize_feat(s)
             quantize_w4(0, s)
             out_1_tile(s, "SSVS")
+
+        def prepare_h3(s):
+            r, step = divmod(s + 3, 4)
+            if 2 <= r < 4 and step < 2:
+                interleave_h3("V", r, step)
+            if 2 <= r < 4 and step == 2:
+                quantize_h3(r)
+
+        s = 2
         for unit in range(4, 16):
-            q, g = divmod(unit, 4)
-            s = unit - 2
             q0, t0 = divmod(unit - FIRST_MIXED, 4)
-            turn_w4(q, g)
+            turn_w4(*divmod(unit, 4))
             if unit > FIRST_MIXED:
                 finish_out_0(unit - 1 - FIRST_MIXED, "V")
             if FIRST_SORTED <= unit + 1 < 16:
@@ -375,31 +377,30 @@ def tile_additivecoupling_pa_v_kernel(tc, x, h3, W4, b4, W5, b5, z4, grad_out, o
             if unit == 5:
                 quantize_feat(3)
             for a in range(4):
-                out_1_bank(s, a, ("VSSS" if unit >= FIRST_MIXED else "SVSS")[a], slots[s // 2])
+                out_1_bank(s, a, ("VSSS" if unit >= FIRST_MIXED else "SVSS")[a], halves[s])
                 if a == 0 and unit > 4:
                     quantize_w4(*divmod(unit - 1, 4))
             if unit >= FIRST_MIXED:
                 for a in range(4):
                     out_0_pass(t0, q0, a)
-            if s >= 4:
-                store_out_1(s, 1)
-            elif s % 2 == 1:
-                store_out_1(s - 1, 2)
+            store_out_1(s)
             if unit == 4:
                 interleave_h3("V", 1, 1)
                 quantize_feat(2)
                 quantize_h3(1)
-            if unit in (7, 8, 11, 12):
-                interleave_h3("V", (unit + 1) // 4, (unit + 1) % 4)
-            if unit in (9, 13):
-                quantize_h3(q)
+            prepare_h3(s)
+            s += 1
+            if unit in TWO_TILES:
+                out_1_tile(s)
+                prepare_h3(s)
+                s += 1
         quantize_w4(3, 3)
         done = 16 - FIRST_MIXED
         finish_out_0(done - 1, "V")
-        split.append(0)
         for i in range(done, 16):
-            if i - done < 2:
-                out_1_tile(14 + i - done)
+            if s < 16:
+                out_1_tile(s)
+                s += 1
             for g in range(4):
                 out_0_pass(i % 4, i // 4, g)
             finish_out_0(i, "SV"[i % 2])

@@ -28,7 +28,7 @@ def tile_additivecoupling_pa_v_kernel(tc, x, h3, W4, b4, W5, b5, z4, grad_out, o
     with ExitStack() as ctx:
         const = ctx.enter_context(tc.tile_pool(name="const", bufs=1))
         big = ctx.enter_context(tc.tile_pool(name="big", bufs=1))
-        small = ctx.enter_context(tc.tile_pool(name="small", bufs=12))
+        small = ctx.enter_context(tc.tile_pool(name="small", bufs=11))
         psum = ctx.enter_context(tc.psum_pool(name="psum", bufs=1))
         ctx.enter_context(tc.manual_schedule())
 
@@ -102,17 +102,11 @@ def tile_additivecoupling_pa_v_kernel(tc, x, h3, W4, b4, W5, b5, z4, grad_out, o
 
         z4_rows = z4.rearrange("(p j) o -> p j o", j=J)
         grad_rows = grad_out.rearrange("(p j) d -> p j d", j=J)
-        raw_grad, raw_w5, raw_z4, raw_w4, raw_w4_whole = {}, {}, {}, {}, {}
+        raw_w5, raw_z4, raw_w4, raw_w4_whole = {}, {}, {}, {}
 
-        def load_grad(pair):
-            offset = SLOT * SLOT_DZ1 + SLOT // 4 * pair
-            raw_grad[pair] = load([P, 2, 2 * HALF], BF16, "raw_grad_%d" % pair, offset, grad_rows[:, 2 * pair : 2 * pair + 2, :])
-
-        def load_w5(first, count):
-            rows = W5[N * first : N * (first + count), :].rearrange("(a p j) k -> p a j k", a=count, j=J)
-            raw = load([P, count, J, HALF], BF16, "raw_w5_%d" % first, SLOT * SLOT_W5 + SLOT // 4 * first, rows)
-            for a in range(count):
-                raw_w5[first + a] = raw[:, a, :, :]
+        def load_w5(half):
+            rows = W5[2 * N * half : 2 * N * (half + 1), :].rearrange("(p j) k -> p j k", j=2 * J)
+            raw_w5[half] = load([P, 2 * J, HALF], BF16, "raw_w5_%d" % half, SLOT * SLOT_W5 + SLOT // 2 * half, rows)
 
         def load_z4(half, pair):
             source = z4_rows[:, 2 * pair : 2 * pair + 2, 2 * N * half : 2 * N * (half + 1)]
@@ -127,11 +121,9 @@ def tile_additivecoupling_pa_v_kernel(tc, x, h3, W4, b4, W5, b5, z4, grad_out, o
             for j in range(count):
                 raw_w4[q, first + j] = raw[:, j, :]
 
-        load_grad(0)
-        load_grad(1)
-        load_w5(0, 1)
-        load_w5(1, 1)
-        load_w5(2, 2)
+        load_w5(0)
+        raw_grad = load([P, J, 2 * HALF], BF16, "raw_grad", SLOT * SLOT_DZ1, grad_rows)
+        load_w5(1)
         load_z4(0, 0)
         load_z4(0, 1)
         load_z4(1, 0)
@@ -139,19 +131,37 @@ def tile_additivecoupling_pa_v_kernel(tc, x, h3, W4, b4, W5, b5, z4, grad_out, o
         raw_h3 = load([P, J, MID], BF16, "raw_h3", SLOT * SLOT_H3, h3.rearrange("(p j) i -> p j i", j=J))
         load_w4(0, SLOT_W4, 0, 2)
         load_w4(0, SLOT_W4, 2, 2)
-        load_w4(1, SLOT_W4 + 1, 0, 4)
 
         dz2_grouped = new_grouped("dz2_grouped")
-        for pair in range(2):
-            even = const.tile([P, 2, HALF], BF16, name="even_%d" % pair, align_bytes=64)
-            even_cols = raw_grad[pair][:].rearrange("p j (k two) -> p j k two", two=2)[:, :, :, 0]
-            nc.vector.tensor_copy(out=even[:], in_=even_cols)
-            turn_pair(dz2_grouped, pair, [even[:, 0, :], even[:, 1, :]], "S", "dz2_grouped")
 
-        def turn_w5(a, engines):
-            return turn([raw_w5[a][:, j, :] for j in range(J)], engines, "w5_grouped_%d" % a)
-        def quantize_w5(a, grouped):
-            quantize(grouped, w5_codes[:, a, :], w5_scales[:, a, :], E4M3)
+        def turn_dz2(pair, engines):
+            even = small.tile([P, 2, HALF], BF16, tag="grouped", name="even_%d" % pair, align_bytes=64)
+            even_cols = raw_grad[:, 2 * pair : 2 * pair + 2, :].rearrange("p j (k two) -> p j k two", two=2)[:, :, :, 0]
+            copy(engines[0], even[:], even_cols)
+            turn_pair(dz2_grouped, pair, [even[:, 0, :], even[:, 1, :]], engines[1], "dz2_grouped")
+
+        w5_grouped = {}
+
+        def turn_w5(half, pairs, engines):
+            if half not in w5_grouped:
+                offset = SLOT * (SLOT_W4 + 1) + SLOT // 2 * half
+                w5_grouped[half] = big_tile([P, P, 2 * J, 2], F32, "w5_grouped_%d" % half, offset)
+            grouped = w5_grouped[half]
+            for pair in pairs:
+                words = every_second([raw_w5[half][:, j, :] for j in (2 * pair, 2 * pair + 1)])
+                bank = turn_bank("w5_grouped_%d_bank_%d" % (half, pair))
+                for i in range(2):
+                    for u in range(2):
+                        nc.tensor.transpose(bank[:, i, u, :], words[i][u], ident[:])
+                copy(engines[pair], grouped[:, :, 2 * pair : 2 * pair + 2, :], bank[:].rearrange("p i u m -> p m i u"))
+
+        def quantize_w5(a):
+            rows = w5_grouped[a // 2][:, P // 2 * (a % 2) : P // 2 * (a % 2 + 1), :, :]
+            nc.vector.quantize_mx(
+                out=w5_codes[:, a, :].bitcast(E4M3),
+                scales=w5_scales[:, a, :],
+                in_=rows.rearrange("p m j u -> p (m j u)").bitcast(BF16),
+            )
 
         dz1 = {}
 
@@ -170,10 +180,10 @@ def tile_additivecoupling_pa_v_kernel(tc, x, h3, W4, b4, W5, b5, z4, grad_out, o
             )
             saved = raw_z4[a // 2, t // 2][:, t % 2, N * (a % 2) : N * (a % 2 + 1)]
             nc.vector.scalar_tensor_tensor(
-                out=dz1[a][:, t, :].rearrange("p (m j) -> p m j", j=J),
-                in0=saved.rearrange("p (m j) -> p m j", j=J),
+                out=dz1[a][:, t, :],
+                in0=saved,
                 scalar=0.0,
-                in1=dh[:].rearrange("p (j m) -> p m j", j=J),
+                in1=dh[:],
                 op0=ALU.is_gt,
                 op1=ALU.mult,
             )
@@ -245,10 +255,11 @@ def tile_additivecoupling_pa_v_kernel(tc, x, h3, W4, b4, W5, b5, z4, grad_out, o
         out_0_rows = out_0.rearrange("(p t) i -> p t i", t=J)
         staged_1, staged_0 = {}, {}
 
-        def out_1_bank(s, a, engine, half_slot):
+        def out_1_bank(s, a, engine):
             r, e = divmod(s, J)
-            if s not in staged_1:
-                staged_1[s] = big_tile([P, MID], F32, "out_1_rows_%d" % s, SLOT // 2 * half_slot)
+            first, count, half_slot = [group for group in OUT_1_GROUPS if group[0] <= s][-1]
+            if first not in staged_1:
+                staged_1[first] = big_tile([P, count, MID], F32, "out_1_rows_%d" % first, SLOT // 2 * half_slot)
             acc = sum_bank("out_1_%d_%d" % (s, a))
             nc.tensor.matmul_mx(
                 out=acc[:],
@@ -259,10 +270,12 @@ def tile_additivecoupling_pa_v_kernel(tc, x, h3, W4, b4, W5, b5, z4, grad_out, o
                 start=True,
                 stop=True,
             )
-            copy(engine, staged_1[s][:, N * a : N * (a + 1)], acc[:])
+            copy(engine, staged_1[first][:, s - first, N * a : N * (a + 1)], acc[:])
 
         def store_out_1(s):
-            nc.sync.dma_start(out=out_1_rows[s // 2, :, s % 2, :], in_=staged_1[s][:])
+            first, count, half_slot = [group for group in OUT_1_GROUPS if group[0] <= s][-1]
+            if s == first + count - 1:
+                nc.sync.dma_start(out=out_1_rows[first // 2, :, first % 2 : first % 2 + count, :], in_=staged_1[first][:])
 
         open_sums = {}
 
@@ -280,9 +293,10 @@ def tile_additivecoupling_pa_v_kernel(tc, x, h3, W4, b4, W5, b5, z4, grad_out, o
             )
 
         def out_0_copy(t, q, engine):
-            if q not in staged_0:
-                staged_0[q] = big_tile([P, J, N], F32, "out_0_cols_%d" % q, SLOT * SLOT_W4 + SLOT // 2 * (q % 2))
-            rows = staged_0[q][:, t, :]
+            first, count, half_slot = [group for group in OUT_0_GROUPS if group[0] <= t][-1]
+            if first not in staged_0:
+                staged_0[first] = big_tile([P, count, MID], F32, "out_0_rows_%d" % first, SLOT // 2 * half_slot)
+            rows = staged_0[first][:, t - first, N * q : N * (q + 1)]
             copy(engine, rows.rearrange("p (m j) -> p m j", j=J), open_sums[t, q][:].rearrange("p (j m) -> p m j", j=J))
 
         def out_0_bank(t, q, engine):
@@ -290,27 +304,31 @@ def tile_additivecoupling_pa_v_kernel(tc, x, h3, W4, b4, W5, b5, z4, grad_out, o
                 out_0_pass(t, q, g)
             out_0_copy(t, q, engine)
 
-        def store_out_0(q, first, count):
-            tiles = slice(first, first + count)
-            nc.sync.dma_start(out=out_0_rows[:, tiles, N * q : N * (q + 1)], in_=staged_0[q][:, tiles, :])
+        def store_out_0(first, count, cols):
+            nc.sync.dma_start(out=out_0_rows[:, first : first + count, cols], in_=staged_0[first][:, :, cols])
 
-        w5_grouped = {0: turn_w5(0, "VS")}
+        turn_w5(0, range(J), "SVSS")
+        turn_dz2(0, "VS")
+        turn_dz2(1, "VV")
+        quantize_w5(0)
         quantize(dz2_grouped, dz2_codes[:], dz2_scales[:], E5M2)
-        w5_grouped[1] = turn_w5(1, "VS")
-        quantize_w5(0, w5_grouped[0])
-        w5_grouped[2] = turn_w5(2, "SS")
-        quantize_w5(1, w5_grouped[1])
+        turn_w5(1, (0, 1), "SSSS")
+        quantize_w5(1)
         make_dz1(0, 0)
         make_dz1(0, 1)
-        w5_grouped[3] = turn_w5(3, "SS")
-        load_w4(2, SLOT_W5, 0, 4)
-        quantize_w5(2, w5_grouped[2])
+        turn_w5(1, (2, 3), "SSSS")
         make_dz1(0, 2)
         make_dz1(0, 3)
-        make_dz1_chunk(1)
+        quantize_w5(2)
+        make_dz1(1, 0)
+        make_dz1(1, 1)
+        make_dz1(1, 2)
+        make_dz1(1, 3)
         interleave_tok("S", 0)
         turn_dz1(0)
-        quantize_w5(3, w5_grouped[3])
+        quantize_w5(3)
+        load_w4(1, SLOT_W4 + 1, 0, 4)
+        load_w4(2, SLOT_W5, 0, 4)
         make_dz1_chunk(2)
         interleave_tok("S", 1, 0, 2)
         turn_dz1(1)
@@ -322,10 +340,10 @@ def tile_additivecoupling_pa_v_kernel(tc, x, h3, W4, b4, W5, b5, z4, grad_out, o
         turn_dz1(3)
         interleave_h3("S", 0, 0)
         quantize_tok(0)
+        quantize_tok(1)
         interleave_tok("V", 3)
         for g in range(4):
             turn_w4(0, g, (0,))
-        quantize_tok(1)
         interleave_h3("V", 0, 1)
         quantize_tok(2)
         quantize_h3(0)
@@ -334,42 +352,34 @@ def tile_additivecoupling_pa_v_kernel(tc, x, h3, W4, b4, W5, b5, z4, grad_out, o
             turn_w4(0, g, (1,))
         interleave_h3("V", 1, 0)
 
-        Z, D, W, H = 2 * SLOT_Z4 + 2, 2 * SLOT_DZ1, 2 * SLOT_W4, 2 * SLOT_H3
-        halves = [Z, Z + 1, D, D + 1, W + 1, W + 2, W + 3, Z, Z + 1, D, D + 1, W + 2, W + 3, 0, 1, H]
+        Z, D, W, H, X = 2 * SLOT_Z4 + 2, 2 * SLOT_DZ1, 2 * SLOT_W4, 2 * SLOT_H3, 14
+        OUT_1_GROUPS = [(0, 2, Z), (2, 2, D), (4, 1, X), (5, 1, W + 2), (6, 2, Z), (8, 2, D), (10, 2, W + 2), (12, 2, 0), (14, 1, H), (15, 1, H + 1)]
+        OUT_0_GROUPS = [(0, 2, W), (2, 1, X), (3, 1, W + 3)]
+        FIRST_SORTED = 8
+        EARLY_SUMS = {7: (0, 0), 9: (1, 0), 10: (0, 1), 12: (1, 1), 13: (0, 2), 14: (1, 2), 15: (2, 0)}
+        TWO_TILES = (8, 11)
 
         def out_1_tile(s, engines="VSVS"):
             for a in range(4):
-                out_1_bank(s, a, engines[a], halves[s])
+                out_1_bank(s, a, engines[a])
             store_out_1(s)
 
-        def finish_out_0(i, engine):
-            out_0_copy(i % 4, i // 4, engine)
-            if i % 4 == 3 and i < 12:
-                store_out_0(i // 4, 0, 4)
-            if i == 13:
-                store_out_0(3, 0, 2)
-            if i > 13:
-                store_out_0(3, i % 4, 1)
-
-        FIRST_SORTED, FIRST_MIXED, TWO_TILES = 8, 7, (9, 13)
-        for s in range(2):
-            quantize_feat(s)
-            quantize_w4(0, s)
-            out_1_tile(s, "SSVS")
-
         def prepare_h3(s):
-            r, step = divmod(s + 3, 4)
+            r, step = divmod(s + 4, 4)
             if 2 <= r < 4 and step < 2:
                 interleave_h3("V", r, step)
             if 2 <= r < 4 and step == 2:
                 quantize_h3(r)
 
+        for s in range(2):
+            quantize_feat(s)
+            quantize_w4(0, s)
+            out_1_tile(s, "SSVS")
         s = 2
         for unit in range(4, 16):
-            q0, t0 = divmod(unit - FIRST_MIXED, 4)
             turn_w4(*divmod(unit, 4))
-            if unit > FIRST_MIXED:
-                finish_out_0(unit - 1 - FIRST_MIXED, "V")
+            if unit - 1 in EARLY_SUMS:
+                out_0_copy(*EARLY_SUMS[unit - 1], "V")
             if FIRST_SORTED <= unit + 1 < 16:
                 sort_w4(*divmod(unit + 1, 4))
             if unit in (5, 6):
@@ -377,12 +387,12 @@ def tile_additivecoupling_pa_v_kernel(tc, x, h3, W4, b4, W5, b5, z4, grad_out, o
             if unit == 5:
                 quantize_feat(3)
             for a in range(4):
-                out_1_bank(s, a, ("VSSS" if unit >= FIRST_MIXED else "SVSS")[a], halves[s])
+                out_1_bank(s, a, ("VSSS" if unit >= 7 else "SVSS")[a])
                 if a == 0 and unit > 4:
                     quantize_w4(*divmod(unit - 1, 4))
-            if unit >= FIRST_MIXED:
-                for a in range(4):
-                    out_0_pass(t0, q0, a)
+            if unit in EARLY_SUMS:
+                for g in range(4):
+                    out_0_pass(*EARLY_SUMS[unit], g)
             store_out_1(s)
             if unit == 4:
                 interleave_h3("V", 1, 1)
@@ -395,12 +405,17 @@ def tile_additivecoupling_pa_v_kernel(tc, x, h3, W4, b4, W5, b5, z4, grad_out, o
                 prepare_h3(s)
                 s += 1
         quantize_w4(3, 3)
-        done = 16 - FIRST_MIXED
-        finish_out_0(done - 1, "V")
-        for i in range(done, 16):
-            if s < 16:
-                out_1_tile(s)
-                s += 1
-            for g in range(4):
-                out_0_pass(i % 4, i // 4, g)
-            finish_out_0(i, "SV"[i % 2])
+        if 15 in EARLY_SUMS:
+            out_0_copy(*EARLY_SUMS[15], "V")
+        for s in range(s, 16):
+            out_1_tile(s)
+        left = [(t, q) for t in range(J) for q in range(4) if (t, q) not in EARLY_SUMS.values()]
+        left.sort(key=lambda tq: (tq[0] // 2 * 2 if tq[0] < 2 else tq[0], tq[1], tq[0]))
+        for i, (t, q) in enumerate(left):
+            out_0_bank(t, q, "SV"[i % 2])
+            if (t, q) == (1, 3):
+                store_out_0(0, 2, slice(0, MID))
+            if (t, q) == (2, 3):
+                store_out_0(2, 1, slice(0, MID))
+            if t == 3 and q > 0:
+                store_out_0(3, 1, slice(0 if q == 1 else N * q, N * (q + 1)))

@@ -35,16 +35,16 @@ def tile_additivecoupling_pa_v_kernel(tc, x, h3, W4, b4, W5, b5, z4, grad_out, o
         ident = const.tile([P, P], F32, name="ident")
         make_identity(nc, ident[:])
 
-        def mx_tiles(name, tag):
-            codes = const.tile([P, 4, N], U32, tag=tag + "_codes", name=name + "_codes", align_bytes=64)
-            scales = const.tile([P, 4, N], U8, tag=tag + "_scales", name=name + "_scales", align_bytes=64)
-            return codes, scales
+        def mx_tiles(name, tag, shift=128):
+            codes = const.tile([P, 4, N], U32, tag=tag + "_codes", name=name + "_codes", align_bytes=256)
+            room = const.tile([P, 4 * N + 256], U8, tag=tag + "_scales", name=name + "_scales", align_bytes=256)
+            return codes, room[:, shift : shift + 4 * N].rearrange("p (g n) -> p g n", g=4)
 
-        dz2_codes = const.tile([P, N], U32, name="dz2_codes", align_bytes=64)
-        dz2_scales = const.tile([P, N], U8, name="dz2_scales", align_bytes=64)
-        h3_codes, h3_scales = mx_tiles("h3", "h3")
+        dz2_room = mx_tiles("dz2", "w4_2")
+        dz2_codes, dz2_scales = dz2_room[0][:, 0, :], dz2_room[1][:, 0, :]
+        h3_codes, h3_scales = mx_tiles("h3", "h3", 64)
         tok_codes, tok_scales = mx_tiles("tok", "tok")
-        feat_codes, feat_scales = mx_tiles("feat", "feat")
+        feat_codes, feat_scales = mx_tiles("feat", "feat", 64)
         w5_codes, w5_scales = mx_tiles("w5", "last")
 
         banks_taken = []
@@ -311,7 +311,7 @@ def tile_additivecoupling_pa_v_kernel(tc, x, h3, W4, b4, W5, b5, z4, grad_out, o
         turn_dz2(0, "VS")
         turn_dz2(1, "VV")
         quantize_w5(0)
-        quantize(dz2_grouped, dz2_codes[:], dz2_scales[:], E5M2)
+        quantize(dz2_grouped, dz2_codes, dz2_scales, E5M2)
         turn_w5(1, (0, 1), "SSSS")
         quantize_w5(1)
         make_dz1(0, 0)

@@ -353,8 +353,8 @@ def tile_additivecoupling_pa_v_kernel(tc, x, h3, W4, b4, W5, b5, z4, grad_out, o
         interleave_h3("V", 1, 0)
 
         Z, D, W, H, X = 2 * SLOT_Z4 + 2, 2 * SLOT_DZ1, 2 * SLOT_W4, 2 * SLOT_H3, 14
-        OUT_1_GROUPS = [(0, 2, Z), (2, 2, D), (4, 1, X), (5, 1, W + 2), (6, 2, Z), (8, 2, D), (10, 2, W + 2), (12, 2, 0), (14, 1, H), (15, 1, H + 1)]
-        OUT_0_GROUPS = [(0, 2, W), (2, 1, X), (3, 1, W + 3)]
+        OUT_1_GROUPS = [(0, 2, Z), (2, 2, D), (4, 1, X), (5, 1, W + 2), (6, 2, Z), (8, 2, D), (10, 2, W + 2), (12, 1, 0), (13, 1, 1), (14, 1, H), (15, 1, H + 1)]
+        OUT_0_GROUPS = [(0, 1, W), (1, 1, W + 1), (2, 1, X), (3, 1, W + 3)]
         FIRST_SORTED = 8
         EARLY_SUMS = {7: (0, 0), 9: (1, 0), 10: (0, 1), 12: (1, 1), 13: (0, 2), 14: (1, 2), 15: (2, 0)}
         TWO_TILES = (8, 11)
@@ -413,9 +413,7 @@ def tile_additivecoupling_pa_v_kernel(tc, x, h3, W4, b4, W5, b5, z4, grad_out, o
         left.sort(key=lambda tq: (tq[0] // 2 * 2 if tq[0] < 2 else tq[0], tq[1], tq[0]))
         for i, (t, q) in enumerate(left):
             out_0_bank(t, q, "SV"[i % 2])
-            if (t, q) == (1, 3):
-                store_out_0(0, 2, slice(0, MID))
-            if (t, q) == (2, 3):
-                store_out_0(2, 1, slice(0, MID))
+            if t < 3 and q == 3:
+                store_out_0(t, 1, slice(0, MID))
             if t == 3 and q > 0:
                 store_out_0(3, 1, slice(0 if q == 1 else N * q, N * (q + 1)))

@@ -353,8 +353,8 @@ def tile_additivecoupling_pa_v_kernel(tc, x, h3, W4, b4, W5, b5, z4, grad_out, o
         interleave_h3("V", 1, 0)
 
         Z, D, W, H, X = 2 * SLOT_Z4 + 2, 2 * SLOT_DZ1, 2 * SLOT_W4, 2 * SLOT_H3, 14
-        OUT_1_GROUPS = [(0, 2, Z), (2, 2, D), (4, 1, X), (5, 1, W + 2), (6, 2, Z), (8, 2, D), (10, 2, W + 2), (12, 1, 0), (13, 1, 1), (14, 1, H), (15, 1, H + 1)]
-        OUT_0_GROUPS = [(0, 1, W), (1, 1, W + 1), (2, 1, X), (3, 1, W + 3)]
+        OUT_1_GROUPS = [(0, 2, Z), (2, 2, D), (4, 1, X), (5, 1, W + 2), (6, 2, Z), (8, 1, W + 3), (9, 1, D), (10, 1, 0), (11, 1, 1), (12, 1, W + 2), (13, 1, D + 1), (14, 1, H), (15, 1, H + 1)]
+        OUT_0_GROUPS = [(0, 1, W), (1, 1, W + 1), (2, 1, X), (3, 1, Z)]
         FIRST_SORTED = 8
         EARLY_SUMS = {7: (0, 0), 9: (1, 0), 10: (0, 1), 12: (1, 1), 13: (0, 2), 14: (1, 2), 15: (2, 0)}
         TWO_TILES = (8, 11)

@@ -22,13 +22,15 @@ SLOT = 16384
 
 SLOT_W5, SLOT_Z4, SLOT_DZ1, SLOT_H3, SLOT_W4 = 0, 1, 3, 4, 5
 
+CELL = 4096
+
 
 def tile_additivecoupling_pa_v_kernel(tc, x, h3, W4, b4, W5, b5, z4, grad_out, out_0, out_1):
     nc = tc.nc
     with ExitStack() as ctx:
         const = ctx.enter_context(tc.tile_pool(name="const", bufs=1))
         big = ctx.enter_context(tc.tile_pool(name="big", bufs=1))
-        small = ctx.enter_context(tc.tile_pool(name="small", bufs=11))
+        small = ctx.enter_context(tc.tile_pool(name="small", bufs=1))
         psum = ctx.enter_context(tc.psum_pool(name="psum", bufs=1))
         ctx.enter_context(tc.manual_schedule())
 
@@ -76,8 +78,19 @@ def tile_additivecoupling_pa_v_kernel(tc, x, h3, W4, b4, W5, b5, z4, grad_out, o
         def quantize(grouped, codes, scales, fmt):
             nc.vector.quantize_mx(out=codes.bitcast(fmt), scales=scales, in_=grouped[:].rearrange("p c t -> p (c t)"))
 
+        CELLS = {"even_0": 0, "even_1": 1, "dz2_grouped": 2}
+        CELLS.update({"feat_grouped_%d" % a: 3 + a for a in range(4)})
+        CELLS.update({"tok_grouped_%d" % a: 7 + a for a in range(4)})
+        CELLS.update({"h3_grouped_%d" % r: (0, 9)[r % 2] for r in range(4)})
+        CELLS.update({"w4_grouped_%d_%d" % divmod(unit, 4): (1, 2, 7, 8, 10)[unit] for unit in range(5)})
+        CELLS.update({"w4_grouped_%d_%d" % divmod(unit, 4): 3 + unit % 4 for unit in range(5, 16)})
+        CELLS.update({"w4_sorted_%d_%d" % divmod(unit, 4): 3 + (unit - 3) % 4 for unit in range(8, 16)})
+
+        def small_tile(shape, dtype, name):
+            return small.tile(shape, dtype, name=name, align_bytes=64, offset=CELL * CELLS[name])
+
         def new_grouped(name):
-            return small.tile([P, N, J], BF16, tag="grouped", name=name, align_bytes=64)
+            return small_tile([P, N, J], BF16, name)
 
         def every_second(rows):
             return [[row.bitcast(F32)[:, u::2] for u in range(2)] for row in rows]
@@ -135,7 +148,7 @@ def tile_additivecoupling_pa_v_kernel(tc, x, h3, W4, b4, W5, b5, z4, grad_out, o
         dz2_grouped = new_grouped("dz2_grouped")
 
         def turn_dz2(pair, engines):
-            even = small.tile([P, 2, HALF], BF16, tag="grouped", name="even_%d" % pair, align_bytes=64)
+            even = small_tile([P, 2, HALF], BF16, "even_%d" % pair)
             even_cols = raw_grad[:, 2 * pair : 2 * pair + 2, :].rearrange("p j (k two) -> p j k two", two=2)[:, :, :, 0]
             copy(engines[0], even[:], even_cols)
             turn_pair(dz2_grouped, pair, [even[:, 0, :], even[:, 1, :]], engines[1], "dz2_grouped")
@@ -230,9 +243,9 @@ def tile_additivecoupling_pa_v_kernel(tc, x, h3, W4, b4, W5, b5, z4, grad_out, o
         w4_sorted = {}
 
         def sort_w4(q, g):
-            words = small.tile([P, J, 2, P], F32, tag="grouped", name="w4_sorted_%d_%d" % (q, g), align_bytes=64)
-            source = raw_w4_whole[q][:, :, N * g : N * (g + 1)].bitcast(F32)
-            nc.vector.tensor_copy(out=words[:], in_=source.rearrange("p j (w u) -> p j u w", u=2))
+            words = small_tile([P, J, 2, P], F32, "w4_sorted_%d_%d" % (q, g))
+            source = raw_w4_whole[q][:, :, N * g : N * (g + 1)].bitcast(U32)
+            nc.gpsimd.tensor_copy(out=words[:].bitcast(U32), in_=source.rearrange("p j (w u) -> p j u w", u=2))
             w4_sorted[q, g] = words
 
         def turn_w4(q, g, pairs=(0, 1), engines="SS"):
@@ -380,8 +393,6 @@ def tile_additivecoupling_pa_v_kernel(tc, x, h3, W4, b4, W5, b5, z4, grad_out, o
             turn_w4(*divmod(unit, 4))
             if unit - 1 in EARLY_SUMS:
                 out_0_copy(*EARLY_SUMS[unit - 1], "V")
-            if FIRST_SORTED <= unit + 1 < 16:
-                sort_w4(*divmod(unit + 1, 4))
             if unit in (5, 6):
                 quantize_w4(0, unit - 3)
             if unit == 5:
@@ -390,6 +401,8 @@ def tile_additivecoupling_pa_v_kernel(tc, x, h3, W4, b4, W5, b5, z4, grad_out, o
                 out_1_bank(s, a, ("VSSS" if unit >= 7 else "SVSS")[a])
                 if a == 0 and unit > 4:
                     quantize_w4(*divmod(unit - 1, 4))
+                    if FIRST_SORTED <= unit + 2 < 16:
+                        sort_w4(*divmod(unit + 2, 4))
             if unit in EARLY_SUMS:
                 for g in range(4):
                     out_0_pass(*EARLY_SUMS[unit], g)

from contextlib import ExitStack

import concourse.mybir as mybir
from concourse.masks import make_identity

B, HALF, MID = 512, 512, 2048
FLOPS = 2 * B * HALF * MID + 2 * (2 * B * MID * MID)
BYTES = 2 * B * HALF + 2 * MID * HALF + 4 * B * MID + 2 * B * MID + 2 * MID * MID + 4 * B * MID + 4 * MID * MID

F32 = mybir.dt.float32
BF16 = mybir.dt.bfloat16
U32 = mybir.dt.uint32
U8 = mybir.dt.uint8
E4M3 = mybir.dt.float8_e4m3fn_x4
E5M2 = mybir.dt.float8_e5m2_x4
ALU = mybir.AluOpType

P = 128
J = 4
N = 512
SLOT = 16384

SLOT_W5, SLOT_Z4, SLOT_DZ1, SLOT_H3, SLOT_W4 = 0, 1, 3, 4, 5

CELL = 4096


def tile_additivecoupling_pa_v_kernel(tc, x, h3, W4, b4, W5, b5, z4, grad_out, out_0, out_1):
    nc = tc.nc
    with ExitStack() as ctx:
        const = ctx.enter_context(tc.tile_pool(name="const", bufs=1))
        big = ctx.enter_context(tc.tile_pool(name="big", bufs=1))
        small = ctx.enter_context(tc.tile_pool(name="small", bufs=1))
        psum = ctx.enter_context(tc.psum_pool(name="psum", bufs=1))
        ctx.enter_context(tc.manual_schedule())

        ident = const.tile([P, P], F32, name="ident")
        make_identity(nc, ident[:])

        def mx_tiles(name, tag, shift=128):
            codes = const.tile([P, 4, N], U32, tag=tag + "_codes", name=name + "_codes", align_bytes=256)
            room = const.tile([P, 4 * N + 256], U8, tag=tag + "_scales", name=name + "_scales", align_bytes=256)
            return codes, room[:, shift : shift + 4 * N].rearrange("p (g n) -> p g n", g=4)

        dz2_room = mx_tiles("dz2", "w4_2")
        dz2_codes, dz2_scales = dz2_room[0][:, 0, :], dz2_room[1][:, 0, :]
        h3_codes, h3_scales = mx_tiles("h3", "h3", 64)
        tok_codes, tok_scales = mx_tiles("tok", "tok")
        feat_codes, feat_scales = mx_tiles("feat", "feat", 64)
        w5_codes, w5_scales = mx_tiles("w5", "last")

        banks_taken = []

        def next_bank(shape, name):
            banks_taken.append(name)
            return psum.tile(shape, F32, tag="bank_%d" % (len(banks_taken) % 8), name=name)

        def turn_bank(name):
            return next_bank([P, 2, 2, P], name)

        def sum_bank(name):
            return next_bank([P, N], name)

        def copy(engine, out, in_):
            if engine == "S":
                nc.scalar.copy(out=out, in_=in_)
            else:
                nc.vector.tensor_copy(out=out, in_=in_)

        def big_tile(shape, dtype, name, offset):
            return big.tile(shape, dtype, name=name, align_bytes=64, offset=offset)

        def load(shape, dtype, name, offset, source):
            raw = big_tile(shape, dtype, name, offset)
            nc.sync.dma_start(out=raw[:], in_=source)
            return raw

        def quantize(grouped, codes, scales, fmt):
            nc.vector.quantize_mx(out=codes.bitcast(fmt), scales=scales, in_=grouped[:].rearrange("p c t -> p (c t)"))

        CELLS = {"even_0": 0, "even_1": 1, "dz2_grouped": 2}
        CELLS.update({"feat_grouped_%d" % a: 3 + a for a in range(4)})
        CELLS.update({"tok_grouped_%d" % a: 7 + a for a in range(4)})
        CELLS.update({"h3_grouped_%d" % r: (0, 9)[r % 2] for r in range(4)})
        CELLS.update({"w4_grouped_%d_%d" % divmod(unit, 4): (1, 2, 7, 8, 10)[unit] for unit in range(5)})
        CELLS.update({"w4_grouped_%d_%d" % divmod(unit, 4): 3 + unit % 4 for unit in range(5, 16)})
        CELLS.update({"w4_sorted_%d_%d" % divmod(unit, 4): 3 + (unit - 3) % 4 for unit in range(8, 16)})

        def small_tile(shape, dtype, name):
            return small.tile(shape, dtype, name=name, align_bytes=64, offset=CELL * CELLS[name])

        def new_grouped(name):
            return small_tile([P, N, J], BF16, name)

        def every_second(rows):
            return [[row.bitcast(F32)[:, u::2] for u in range(2)] for row in rows]

        def turn_words(grouped, pair, words, engine, name):
            bank = turn_bank("%s_bank_%d" % (name, pair))
            for i in range(2):
                for u in range(2):
                    nc.tensor.transpose(bank[:, i, u, :], words[i][u], ident[:])
            out_words = grouped[:].rearrange("p c t -> p (c t)").bitcast(F32)
            half = out_words[:, N * pair : N * (pair + 1)].rearrange("p (i r u) -> p i r u", i=2, u=2)
            copy(engine, half, bank[:].rearrange("p i u r -> p i r u"))

        def turn_pair(grouped, pair, rows, engine, name):
            turn_words(grouped, pair, every_second(rows), engine, name)

        def turn(rows, engines, name):
            grouped = new_grouped(name)
            for pair in range(2):
                turn_pair(grouped, pair, rows[2 * pair : 2 * pair + 2], engines[pair], name)
            return grouped

        z4_rows = z4.rearrange("(p j) o -> p j o", j=J)
        grad_rows = grad_out.rearrange("(p j) d -> p j d", j=J)
        raw_w5, raw_z4, raw_w4, raw_w4_whole = {}, {}, {}, {}

        def load_w5(half):
            rows = W5[2 * N * half : 2 * N * (half + 1), :].rearrange("(p j) k -> p j k", j=2 * J)
            raw_w5[half] = load([P, 2 * J, HALF], BF16, "raw_w5_%d" % half, SLOT * SLOT_W5 + SLOT // 2 * half, rows)

        def load_z4(half, pair):
            source = z4_rows[:, 2 * pair : 2 * pair + 2, 2 * N * half : 2 * N * (half + 1)]
            offset = SLOT * SLOT_Z4 + SLOT // 2 * (2 * half + pair)
            raw_z4[half, pair] = load([P, 2, 2 * N], F32, "raw_z4_%d_%d" % (half, pair), offset, source)

        def load_w4(q, slot, first, count):
            rows = W4[N * q : N * (q + 1), :].rearrange("(p j) o -> p j o", j=J)
            offset = SLOT * slot + SLOT // J * first
            raw = load([P, count, MID], BF16, "raw_w4_%d_%d" % (q, first), offset, rows[:, first : first + count, :])
            raw_w4_whole[q] = raw
            for j in range(count):
                raw_w4[q, first + j] = raw[:, j, :]

        load_w5(0)
        raw_grad = load([P, J, 2 * HALF], BF16, "raw_grad", SLOT * SLOT_DZ1, grad_rows)
        load_w5(1)
        load_z4(0, 0)
        load_z4(0, 1)
        load_z4(1, 0)
        load_z4(1, 1)
        raw_h3 = load([P, J, MID], BF16, "raw_h3", SLOT * SLOT_H3, h3.rearrange("(p j) i -> p j i", j=J))
        load_w4(0, SLOT_W4, 0, 2)
        load_w4(0, SLOT_W4, 2, 2)

        dz2_grouped = new_grouped("dz2_grouped")

        def turn_dz2(pair, engines):
            even = small_tile([P, 2, HALF], BF16, "even_%d" % pair)
            even_cols = raw_grad[:, 2 * pair : 2 * pair + 2, :].rearrange("p j (k two) -> p j k two", two=2)[:, :, :, 0]
            copy(engines[0], even[:], even_cols)
            turn_pair(dz2_grouped, pair, [even[:, 0, :], even[:, 1, :]], engines[1], "dz2_grouped")

        w5_grouped = {}

        def turn_w5(half, pairs, engines):
            if half not in w5_grouped:
                offset = SLOT * (SLOT_W4 + 1) + SLOT // 2 * half
                w5_grouped[half] = big_tile([P, P, 2 * J, 2], F32, "w5_grouped_%d" % half, offset)
            grouped = w5_grouped[half]
            for pair in pairs:
                words = every_second([raw_w5[half][:, j, :] for j in (2 * pair, 2 * pair + 1)])
                bank = turn_bank("w5_grouped_%d_bank_%d" % (half, pair))
                for i in range(2):
                    for u in range(2):
                        nc.tensor.transpose(bank[:, i, u, :], words[i][u], ident[:])
                copy(engines[pair], grouped[:, :, 2 * pair : 2 * pair + 2, :], bank[:].rearrange("p i u m -> p m i u"))

        def quantize_w5(a):
            rows = w5_grouped[a // 2][:, P // 2 * (a % 2) : P // 2 * (a % 2 + 1), :, :]
            nc.vector.quantize_mx(
                out=w5_codes[:, a, :].bitcast(E4M3),
                scales=w5_scales[:, a, :],
                in_=rows.rearrange("p m j u -> p (m j u)").bitcast(BF16),
            )

        dz1 = {}

        def make_dz1(a, t):
            if a not in dz1:
                dz1[a] = big_tile([P, J, N], BF16, "dz1_%d" % a, SLOT * SLOT_DZ1 + SLOT // 4 * a)
            dh = sum_bank("dh_%d_%d" % (a, t))
            nc.tensor.matmul_mx(
                out=dh[:],
                lhsT=dz2_codes[:, P * t : P * (t + 1)].bitcast(E5M2),
                lhsT_scale=dz2_scales[:, P * t : P * (t + 1)],
                rhs=w5_codes[:, a, :].bitcast(E4M3),
                rhs_scale=w5_scales[:, a, :],
                start=True,
                stop=True,
            )
            saved = raw_z4[a // 2, t // 2][:, t % 2, N * (a % 2) : N * (a % 2 + 1)]
            nc.vector.scalar_tensor_tensor(
                out=dz1[a][:, t, :],
                in0=saved,
                scalar=0.0,
                in1=dh[:],
                op0=ALU.is_gt,
                op1=ALU.mult,
            )

        feat_grouped = {}

        def turn_dz1(a, engines="SS"):
            feat_grouped[a] = turn([dz1[a][:, t, :] for t in range(J)], engines, "feat_grouped_%d" % a)

        def make_dz1_chunk(a):
            for t in range(J):
                make_dz1(a, t)

        def quantize_feat(a):
            quantize(feat_grouped[a], feat_codes[:, a, :], feat_scales[:, a, :], E5M2)

        tok_grouped = {}

        def interleave_tok(engine, a, part=0, parts=1):
            if part == 0:
                tok_grouped[a] = new_grouped("tok_grouped_%d" % a)
            cols = slice(N // parts * part, N // parts * (part + 1))
            out = tok_grouped[a][:, cols, :].rearrange("p (c i) t -> p c t i", i=4)
            copy(engine, out, dz1[a][:, :, cols].rearrange("p t (c i) -> p c t i", i=4))

        def quantize_tok(a):
            quantize(tok_grouped[a], tok_codes[:, a, :], tok_scales[:, a, :], E5M2)

        h3_grouped = {}

        def interleave_h3(engine, r, half):
            if half == 0:
                h3_grouped[r] = new_grouped("h3_grouped_%d" % r)
            cols = slice(N // 2 * half, N // 2 * (half + 1))
            source = raw_h3[:, :, N * r : N * (r + 1)][:, :, cols]
            out = h3_grouped[r][:, cols, :].rearrange("p (e m i) t -> p m t i e", e=2, i=2)
            copy(engine, out, source.rearrange("p t (m i e) -> p m t i e", e=2, i=2))

        def quantize_h3(r):
            quantize(h3_grouped[r], h3_codes[:, r, :], h3_scales[:, r, :], E4M3)

        w4_codes, w4_scales, w4_grouped = {}, {}, {}

        w4_sorted = {}

        def sort_w4(q, g):
            words = small_tile([P, J, 2, P], F32, "w4_sorted_%d_%d" % (q, g))
            source = raw_w4_whole[q][:, :, N * g : N * (g + 1)].bitcast(U32)
            nc.gpsimd.tensor_copy(out=words[:].bitcast(U32), in_=source.rearrange("p j (w u) -> p j u w", u=2))
            w4_sorted[q, g] = words

        def turn_w4(q, g, pairs=(0, 1), engines="SS"):
            name = "w4_grouped_%d_%d" % (q, g)
            if (q, g) not in w4_grouped:
                w4_grouped[q, g] = new_grouped(name)
            for pair in pairs:
                if (q, g) in w4_sorted:
                    words = [[w4_sorted[q, g][:, j, u, :] for u in range(2)] for j in (2 * pair, 2 * pair + 1)]
                else:
                    words = every_second([raw_w4[q, j][:, N * g : N * (g + 1)] for j in (2 * pair, 2 * pair + 1)])
                turn_words(w4_grouped[q, g], pair, words, engines[pair], name)

        def quantize_w4(q, g):
            if q not in w4_codes:
                w4_codes[q], w4_scales[q] = mx_tiles("w4_%d" % q, "last" if q == 3 else "w4_%d" % q)
            quantize(w4_grouped[q, g], w4_codes[q][:, g, :], w4_scales[q][:, g, :], E4M3)

        out_1_rows = out_1.rearrange("(r p e) o -> r p e o", p=P, e=2)
        out_0_rows = out_0.rearrange("(p t) i -> p t i", t=J)
        staged_1, staged_0 = {}, {}

        def out_1_bank(s, a, engine):
            r, e = divmod(s, J)
            first, count, half_slot = [group for group in OUT_1_GROUPS if group[0] <= s][-1]
            if first not in staged_1:
                staged_1[first] = big_tile([P, count, MID], F32, "out_1_rows_%d" % first, SLOT // 2 * half_slot)
            acc = sum_bank("out_1_%d_%d" % (s, a))
            nc.tensor.matmul_mx(
                out=acc[:],
                lhsT=h3_codes[:, r, P * e : P * (e + 1)].bitcast(E4M3),
                lhsT_scale=h3_scales[:, r, P * e : P * (e + 1)],
                rhs=tok_codes[:, a, :].bitcast(E5M2),
                rhs_scale=tok_scales[:, a, :],
                start=True,
                stop=True,
            )
            copy(engine, staged_1[first][:, s - first, N * a : N * (a + 1)], acc[:])

        def store_out_1(s):
            first, count, half_slot = [group for group in OUT_1_GROUPS if group[0] <= s][-1]
            if s == first + count - 1:
                nc.sync.dma_start(out=out_1_rows[first // 2, :, first % 2 : first % 2 + count, :], in_=staged_1[first][:])

        open_sums = {}

        def out_0_pass(t, q, g):
            if g == 0:
                open_sums[t, q] = sum_bank("out_0_%d_%d" % (t, q))
            nc.tensor.matmul_mx(
                out=open_sums[t, q][:],
                lhsT=feat_codes[:, g, P * t : P * (t + 1)].bitcast(E5M2),
                lhsT_scale=feat_scales[:, g, P * t : P * (t + 1)],
                rhs=w4_codes[q][:, g, :].bitcast(E4M3),
                rhs_scale=w4_scales[q][:, g, :],
                start=(g == 0),
                stop=(g == 3),
            )

        def out_0_copy(t, q, engine):
            first, count, half_slot = [group for group in OUT_0_GROUPS if group[0] <= t][-1]
            if first not in staged_0:
                staged_0[first] = big_tile([P, count, MID], F32, "out_0_rows_%d" % first, SLOT // 2 * half_slot)
            rows = staged_0[first][:, t - first, N * q : N * (q + 1)]
            copy(engine, rows.rearrange("p (m j) -> p m j", j=J), open_sums[t, q][:].rearrange("p (j m) -> p m j", j=J))

        def out_0_bank(t, q, engine):
            for g in range(4):
                out_0_pass(t, q, g)
            out_0_copy(t, q, engine)

        def store_out_0(first, count, cols):
            nc.sync.dma_start(out=out_0_rows[:, first : first + count, cols], in_=staged_0[first][:, :, cols])

        turn_w5(0, range(J), "SVSS")
        turn_dz2(0, "VS")
        turn_dz2(1, "VV")
        quantize_w5(0)
        quantize(dz2_grouped, dz2_codes, dz2_scales, E5M2)
        turn_w5(1, (0, 1), "SSSS")
        quantize_w5(1)
        make_dz1(0, 0)
        make_dz1(0, 1)
        turn_w5(1, (2, 3), "SSSS")
        make_dz1(0, 2)
        make_dz1(0, 3)
        quantize_w5(2)
        make_dz1(1, 0)
        make_dz1(1, 1)
        make_dz1(1, 2)
        make_dz1(1, 3)
        interleave_tok("S", 0)
        turn_dz1(0)
        quantize_w5(3)
        load_w4(1, SLOT_W4 + 1, 0, 4)
        load_w4(2, SLOT_W5, 0, 4)
        make_dz1_chunk(2)
        interleave_tok("S", 1, 0, 2)
        turn_dz1(1)
        make_dz1_chunk(3)
        load_w4(3, SLOT_Z4, 0, 4)
        turn_dz1(2)
        interleave_tok("V", 1, 1, 2)
        interleave_tok("V", 2)
        turn_dz1(3)
        interleave_h3("S", 0, 0)
        quantize_tok(0)
        quantize_tok(1)
        interleave_tok("V", 3)
        for g in range(4):
            turn_w4(0, g, (0,))
        interleave_h3("V", 0, 1)
        quantize_tok(2)
        quantize_h3(0)
        quantize_tok(3)
        for g in range(4):
            turn_w4(0, g, (1,))
        interleave_h3("V", 1, 0)

        Z, D, W, H, X = 2 * SLOT_Z4 + 2, 2 * SLOT_DZ1, 2 * SLOT_W4, 2 * SLOT_H3, 14
        OUT_1_GROUPS = [(0, 2, Z), (2, 2, D), (4, 1, X), (5, 1, W + 2), (6, 2, Z), (8, 1, W + 3), (9, 1, D), (10, 1, 0), (11, 1, 1), (12, 1, W + 2), (13, 1, D + 1), (14, 1, H), (15, 1, H + 1)]
        OUT_0_GROUPS = [(0, 1, W), (1, 1, W + 1), (2, 1, X), (3, 1, Z)]
        FIRST_SORTED = 8
        EARLY_SUMS = {7: (0, 0), 9: (1, 0), 10: (0, 1), 12: (1, 1), 13: (0, 2), 14: (1, 2), 15: (2, 0)}
        TWO_TILES = (8, 11)

        def out_1_tile(s, engines="VSVS"):
            for a in range(4):
                out_1_bank(s, a, engines[a])
            store_out_1(s)

        def prepare_h3(s):
            r, step = divmod(s + 4, 4)
            if 2 <= r < 4 and step < 2:
                interleave_h3("V", r, step)
            if 2 <= r < 4 and step == 2:
                quantize_h3(r)

        for s in range(2):
            quantize_feat(s)
            quantize_w4(0, s)
            out_1_tile(s, "SSVS")
        s = 2
        for unit in range(4, 16):
            turn_w4(*divmod(unit, 4))
            if unit - 1 in EARLY_SUMS:
                out_0_copy(*EARLY_SUMS[unit - 1], "V")
            if unit in (5, 6):
                quantize_w4(0, unit - 3)
            if unit == 5:
                quantize_feat(3)
            for a in range(4):
                out_1_bank(s, a, ("VSSS" if unit >= 7 else "SVSS")[a])
                if a == 0 and unit > 4:
                    quantize_w4(*divmod(unit - 1, 4))
                    if FIRST_SORTED <= unit + 2 < 16:
                        sort_w4(*divmod(unit + 2, 4))
            if unit in EARLY_SUMS:
                for g in range(4):
                    out_0_pass(*EARLY_SUMS[unit], g)
            store_out_1(s)
            if unit == 4:
                interleave_h3("V", 1, 1)
                quantize_feat(2)
                quantize_h3(1)
            prepare_h3(s)
            s += 1
            if unit in TWO_TILES:
                out_1_tile(s)
                prepare_h3(s)
                s += 1
        quantize_w4(3, 3)
        if 15 in EARLY_SUMS:
            out_0_copy(*EARLY_SUMS[15], "V")
        for s in range(s, 16):
            out_1_tile(s)
        left = [(t, q) for t in range(J) for q in range(4) if (t, q) not in EARLY_SUMS.values()]
        left.sort(key=lambda tq: (tq[0] // 2 * 2 if tq[0] < 2 else tq[0], tq[1], tq[0]))
        for i, (t, q) in enumerate(left):
            out_0_bank(t, q, "SV"[i % 2])
            if t < 3 and q == 3:
                store_out_0(t, 1, slice(0, MID))
            if t == 3 and q > 0:
                store_out_0(3, 1, slice(0 if q == 1 else N * q, N * (q + 1)))
